import numpy as np
import ml_dtypes


def mxq(x, axis, fmt="e4m3"):
    dtype, down = {"e4m3": (ml_dtypes.float8_e4m3fn, 7), "e5m2": (ml_dtypes.float8_e5m2, 14)}[fmt]
    v = np.moveaxis(np.asarray(x, np.float32).astype(ml_dtypes.bfloat16).astype(np.float64), axis, -1)
    blocks = v.reshape(v.shape[:-1] + (-1, 32))
    amax = np.abs(blocks).max(-1, keepdims=True)
    byte = np.maximum(np.where(amax > 0, np.frexp(amax)[1] - 1 + 127, 0) - down, 1)
    scale = np.exp2(byte - 127.0)
    codes = (blocks / scale).astype(np.float32).astype(dtype).astype(np.float64)
    return np.moveaxis((codes * scale).reshape(v.shape), -1, axis)


WIDE = False


def mx_kscale(k):
    if not WIDE:
        return np.ones(k)
    levels = np.array([10, -10, 5, -5, 0])
    a = np.random.permutation(np.resize(levels, k // 512 * 4)).reshape(k // 512, 4)
    idx = np.arange(k)
    return np.exp2(a[idx // 512, idx % 128 // 32])


BF16 = ml_dtypes.bfloat16


def bf(x):
    return np.asarray(x, np.float32).astype(BF16)


def f64(x):
    return np.asarray(x).astype(np.float64)


E2M1 = np.array([0.0, 0.5, 1.0, 1.5, 2.0, 3.0, 4.0, 6.0, -0.0, -0.5, -1.0, -1.5, -2.0, -3.0, -4.0, -6.0])


def pack_weight(w, fmt):
    k, n = w.shape
    w = f64(bf(w)).reshape(k // 32, 32, n)
    amax = np.abs(w).max(1)
    if fmt == "e4m3":
        byte = np.frexp(amax)[1] - 1 + 127 - 7
    else:
        mant, ex = np.frexp(amax / 6.0)
        byte = np.where(mant > 0.5, ex, ex - 1) + 127
    byte = np.clip(np.where(amax > 0, byte, 1), 1, 254)
    scaled = (w * np.exp2(127.0 - byte)[:, None, :]).reshape(k, n).astype(np.float32)
    by_word = np.ascontiguousarray(scaled.reshape(k // 512, 128, 4, n).transpose(0, 1, 3, 2))
    if fmt == "e4m3":
        words = by_word.astype(ml_dtypes.float8_e4m3fn).view(np.uint8)
    else:
        c = by_word.astype(ml_dtypes.float4_e2m1fn).view(np.uint8) & 0xF
        words = c[..., 0::2] | (c[..., 1::2] << 4)
    return np.ascontiguousarray(words), np.ascontiguousarray(byte.astype(np.uint8).reshape(k // 512, 16, n))


def unpack_weight(words, scales, fmt):
    g, p, n, _ = words.shape
    if fmt == "e4m3":
        vals = np.ascontiguousarray(words).view(ml_dtypes.float8_e4m3fn).astype(np.float64)
    else:
        nib = np.empty((g, p, n, 4), np.uint8)
        nib[..., 0::2] = words & 0xF
        nib[..., 1::2] = words >> 4
        vals = E2M1[nib]
    vals = vals * np.repeat(np.exp2(scales.astype(np.float64) - 127.0), 8, axis=1)[..., None]
    return vals.transpose(0, 1, 3, 2).reshape(g * 512, n)


B, CIN, R, COUT, H, W, D, KS = 1, 512, 512, 512, 8, 16, 16, 3
P = H * W * D
PAD = (KS - 1) // 2
FMT = "e4m3"


def slice_in_dim(t, a, b, axis):
    idx = [slice(None)] * t.ndim
    idx[axis] = slice(a, b)
    return t[tuple(idx)]


def axis_contract(t, U, axis):
    L = t.shape[axis] - (KS - 1)
    rshape = (1, U.shape[1], 1, 1, 1)
    acc = slice_in_dim(t, 0, L, axis) * U[0].reshape(rshape)
    for k in range(1, KS):
        acc = acc + slice_in_dim(t, k, k + L, axis) * U[k].reshape(rshape)
    return acc


def setup_inputs():
    s, t = mx_kscale(CIN), mx_kscale(R)
    x = bf(np.random.standard_normal((B, CIN, H, W, D)) * s[None, :, None, None, None])
    U_kh = bf(np.random.standard_normal((KS, R)) / np.sqrt(KS))
    U_kw = bf(np.random.standard_normal((KS, R)) / np.sqrt(KS))
    U_kd = bf(np.random.standard_normal((KS, R)) / np.sqrt(KS))
    in_words, in_scales = pack_weight(np.random.standard_normal((CIN, R)) / np.sqrt(CIN) / s[:, None] * t[None, :], FMT)
    out_words, out_scales = pack_weight(np.random.standard_normal((R, COUT)) / np.sqrt(R) / t[:, None], FMT)
    bias = bf(np.random.standard_normal(COUT) * 0.5)
    return {"x": x,
            "U_kh": U_kh,
            "U_kw": U_kw,
            "U_kd": U_kd,
            "U_c_in_words": in_words,
            "U_c_in_scales": in_scales,
            "U_c_out_words": out_words,
            "U_c_out_scales": out_scales,
            "bias": bias}


def reference(x, U_kh, U_kw, U_kd, U_c_in_words, U_c_in_scales, U_c_out_words, U_c_out_scales, bias):
    xq = mxq(f64(x), 1, "e4m3").reshape(B, CIN, P)
    y = (unpack_weight(U_c_in_words, U_c_in_scales, FMT).T @ xq).reshape(B, R, H, W, D)
    y = np.pad(y, ((0, 0), (0, 0), (PAD, PAD), (PAD, PAD), (PAD, PAD)))
    y = axis_contract(y, f64(U_kh), 2)
    y = axis_contract(y, f64(U_kw), 3)
    y = axis_contract(y, f64(U_kd), 4)
    out = (unpack_weight(U_c_out_words, U_c_out_scales, FMT).T @ mxq(y, 1, "e4m3").reshape(B, R, P)).reshape(B, COUT, H, W, D)
    return out + f64(bias)[None, :, None, None, None]

@@ -1,0 +1,246 @@
+from contextlib import ExitStack
+
+import concourse.mybir as mybir
+from concourse.masks import make_identity
+
+F32 = mybir.dt.float32
+BF16 = mybir.dt.bfloat16
+I32 = mybir.dt.int32
+U32 = mybir.dt.uint32
+U8 = mybir.dt.uint8
+FP8X4 = mybir.dt.float8_e4m3fn_x4
+MULT = mybir.AluOpType.mult
+ADD = mybir.AluOpType.add
+COPY = mybir.ActivationFunctionType.Copy
+IDENTITY = mybir.ActivationFunctionType.Identity
+
+P = 128
+PACK = 4
+CHANNELS = 512
+CHUNKS = CHANNELS // P
+H_PLANES, W_ROWS, D_COLS = 8, 16, 16
+PLANE = W_ROWS * D_COLS
+POSITIONS = H_PLANES * PLANE
+SLAB = 2 * PLANE
+SLABS = POSITIONS // SLAB
+TAPS = 3
+BIAS_COLUMN = 3 * TAPS * CHUNKS
+TABLE_COLUMNS = BIAS_COLUMN + CHUNKS
+
+FLOPS = 2 * 2 * CHANNELS * CHANNELS * POSITIONS + (3 * (2 * TAPS - 1) + 1) * CHANNELS * POSITIONS
+
+
+def tap_column(axis, k, j):
+    return (axis * TAPS + k) * CHUNKS + j
+
+
+def load_weight(nc, pool, words_dram, scales_dram, label):
+    words = pool.tile([P, CHANNELS], U32, name=label + "_words", align_bytes=64)
+    plane = pool.tile([P, CHANNELS], U8, name=label + "_plane", align_bytes=64)
+    nc.vector.memset(plane[:].bitcast(I32), 0)
+    for quadrant in range(4):
+        nc.sync.dma_start(
+            out=plane[32 * quadrant : 32 * quadrant + 4, :].bitcast(I32),
+            in_=scales_dram[0, 4 * quadrant : 4 * quadrant + 4, :].bitcast(I32),
+        )
+    nc.sync.dma_start(
+        out=words[:].bitcast(I32),
+        in_=words_dram[0].rearrange("p n t -> p (n t)").bitcast(I32),
+    )
+    return words, plane
+
+
+def tile_lowrankconv3d_kernel(
+    tc, x, U_kh, U_kw, U_kd, U_c_in_words, U_c_in_scales, U_c_out_words, U_c_out_scales, bias, out
+):
+    nc = tc.nc
+    x_rows = x[0].rearrange("(p t) h w d -> p t (h w d)", t=PACK)
+    out_rows = out[0].rearrange("(i m) h w d -> i m (h w d)", m=P)
+
+    with ExitStack() as ctx:
+        keep = ctx.enter_context(tc.tile_pool(name="keep", bufs=1))
+        work = ctx.enter_context(tc.tile_pool(name="work", bufs=2))
+        sums = ctx.enter_context(tc.tile_pool(name="sums", bufs=4))
+        product_banks = ctx.enter_context(tc.psum_pool(name="product_banks", bufs=3))
+        turn_banks = ctx.enter_context(tc.psum_pool(name="turn_banks", bufs=3))
+        out_banks = ctx.enter_context(tc.psum_pool(name="out_banks", bufs=2))
+
+        x_raw = []
+        for s in range(SLABS):
+            x_raw.append(keep.tile([P, PACK, SLAB], BF16, name="x_raw%d" % s))
+        nc.sync.dma_start(out=x_raw[0][:], in_=x_rows[:, :, 0:SLAB])
+        in_words, in_plane = load_weight(nc, keep, U_c_in_words, U_c_in_scales, "u_in")
+        for s in range(1, SLABS):
+            nc.sync.dma_start(out=x_raw[s][:], in_=x_rows[:, :, s * SLAB : (s + 1) * SLAB])
+        out_words, out_plane = load_weight(nc, keep, U_c_out_words, U_c_out_scales, "u_out")
+
+        ident_bf16 = keep.tile([P, P], BF16, name="ident_bf16")
+        make_identity(nc, ident_bf16[:])
+        ident_f32 = keep.tile([P, P], F32, name="ident_f32")
+        make_identity(nc, ident_f32[:])
+
+        table_rows = keep.tile([P, P], BF16, name="table_rows")
+        nc.vector.memset(table_rows[:], 0.0)
+        for axis, taps in enumerate((U_kh, U_kw, U_kd)):
+            first = tap_column(axis, 0, 0)
+            nc.scalar.dma_start(
+                out=table_rows[first : first + TAPS * CHUNKS, :],
+                in_=taps.rearrange("k (j m) -> (k j) m", m=P),
+            )
+        nc.scalar.dma_start(
+            out=table_rows[BIAS_COLUMN:TABLE_COLUMNS, :], in_=bias.rearrange("(i m) -> i m", m=P)
+        )
+        table_bank = turn_banks.tile([P, P], BF16, tag="turn")
+        nc.tensor.transpose(table_bank[:], table_rows[:], ident_bf16[:])
+        table = keep.tile([P, TABLE_COLUMNS], F32, name="table")
+        nc.vector.tensor_copy(out=table[:], in_=table_bank[:, 0:TABLE_COLUMNS])
+
+        def tap(axis, k, j):
+            column = tap_column(axis, k, j)
+            return table[:, column : column + 1]
+
+        after_w = []
+        for j in range(CHUNKS):
+            after_w.append(keep.tile([P, PLANE + POSITIONS], F32, name="after_w%d" % j))
+            nc.vector.memset(after_w[j][:, 0:PLANE], 0.0)
+
+        def quantise_x(s):
+            grouped = work.tile([P, SLAB, PACK], BF16, name="x_grouped", align_bytes=64)
+            source = x_raw[s][:].rearrange("p t (c i) -> p c t i", i=4)
+            target = grouped[:].rearrange("p (c i) t -> p c t i", i=4)
+            if s == 0:
+                nc.vector.tensor_copy(out=target, in_=source)
+            else:
+                nc.scalar.copy(out=target, in_=source)
+            codes = work.tile([P, SLAB], U32, name="x_codes", align_bytes=64)
+            scales = work.tile([P, SLAB], U8, name="x_scales", align_bytes=64)
+            nc.vector.quantize_mx(
+                out=codes[:].bitcast(FP8X4),
+                scales=scales[:],
+                in_=grouped[:].rearrange("p q t -> p (q t)"),
+            )
+            return codes, scales
+
+        def filters_d_and_w(s, j, codes, scales):
+            ranks = slice(j * P, (j + 1) * P)
+            y0 = product_banks.tile([P, SLAB], F32, name="y0")
+            nc.tensor.matmul_mx(
+                out=y0[:],
+                lhsT=in_words[:, ranks].bitcast(FP8X4),
+                lhsT_scale=in_plane[:, ranks],
+                rhs=codes[:].bitcast(FP8X4),
+                rhs_scale=scales[:],
+                start=True,
+                stop=True,
+            )
+            after_d = sums.tile([P, SLAB], F32, name="after_d")
+            nc.scalar.activation(out=after_d[:], in_=y0[:], func=COPY, scale=tap(2, 1, j))
+            y0_rows = y0[:].rearrange("p (r d) -> p r d", d=D_COLS)
+            d_rows = after_d[:].rearrange("p (r d) -> p r d", d=D_COLS)
+            nc.vector.scalar_tensor_tensor(
+                out=d_rows[:, :, 1:D_COLS], in0=y0_rows[:, :, 0 : D_COLS - 1], scalar=tap(2, 0, j),
+                in1=d_rows[:, :, 1:D_COLS], op0=MULT, op1=ADD,
+            )
+            nc.vector.scalar_tensor_tensor(
+                out=d_rows[:, :, 0 : D_COLS - 1], in0=y0_rows[:, :, 1:D_COLS], scalar=tap(2, 2, j),
+                in1=d_rows[:, :, 0 : D_COLS - 1], op0=MULT, op1=ADD,
+            )
+            first = PLANE + s * SLAB
+            result = after_w[j][:, first : first + SLAB]
+            nc.scalar.activation(out=result, in_=after_d[:], func=COPY, scale=tap(1, 1, j))
+            d_planes = after_d[:].rearrange("p (h q) -> p h q", q=PLANE)
+            w_planes = result.rearrange("p (h q) -> p h q", q=PLANE)
+            nc.vector.scalar_tensor_tensor(
+                out=w_planes[:, :, D_COLS:PLANE], in0=d_planes[:, :, 0 : PLANE - D_COLS],
+                scalar=tap(1, 0, j), in1=w_planes[:, :, D_COLS:PLANE], op0=MULT, op1=ADD,
+            )
+            nc.vector.scalar_tensor_tensor(
+                out=w_planes[:, :, 0 : PLANE - D_COLS], in0=d_planes[:, :, D_COLS:PLANE],
+                scalar=tap(1, 2, j), in1=w_planes[:, :, 0 : PLANE - D_COLS], op0=MULT, op1=ADD,
+            )
+
+        def filter_h(s, j, y3):
+            first = PLANE + s * SLAB
+            volume = after_w[j]
+            partial = sums.tile([P, SLAB], F32, name="partial")
+            nc.scalar.activation(
+                out=partial[:], in_=volume[:, first - PLANE : first - PLANE + SLAB], func=COPY,
+                scale=tap(0, 0, j),
+            )
+            above = min(SLAB, POSITIONS - (s * SLAB + PLANE))
+            nc.vector.scalar_tensor_tensor(
+                out=partial[:, 0:above], in0=volume[:, first + PLANE : first + PLANE + above],
+                scalar=tap(0, 2, j), in1=partial[:, 0:above], op0=MULT, op1=ADD,
+            )
+            nc.vector.scalar_tensor_tensor(
+                out=y3[:, j, :], in0=volume[:, first : first + SLAB], scalar=tap(0, 1, j),
+                in1=partial[:], op0=MULT, op1=ADD,
+            )
+
+        def quantise_y3(y3):
+            grouped = work.tile([P, SLAB, PACK], BF16, name="y_grouped", align_bytes=64)
+            grouped_pairs = (
+                grouped[:].rearrange("p q t -> p (q t)").bitcast(F32).rearrange("p (q u) -> p q u", u=2)
+            )
+            for half in range(SLAB // (2 * P)):
+                by_position = turn_banks.tile([P, 2, CHANNELS], BF16, tag="turn")
+                for b in range(2):
+                    q0 = (2 * half + b) * P
+                    for j in range(CHUNKS):
+                        nc.tensor.transpose(
+                            by_position[:, b, j * P : (j + 1) * P], y3[:, j, q0 : q0 + P], ident_bf16[:]
+                        )
+                pairs = work.tile([P, 2, 2, P], F32, name="pairs")
+                nc.scalar.copy(
+                    out=pairs[:], in_=by_position[:].bitcast(F32).rearrange("q b (p u) -> q b u p", u=2)
+                )
+                by_word = turn_banks.tile([P, 2, 2, P], F32, tag="turn")
+                for b in range(2):
+                    for u in range(2):
+                        nc.tensor.transpose(by_word[:, b, u, :], pairs[:, b, u, :], ident_f32[:])
+                nc.scalar.copy(
+                    out=grouped_pairs[:, 2 * half * P : 2 * (half + 1) * P, :].rearrange(
+                        "p (b q) u -> p b q u", b=2
+                    ),
+                    in_=by_word[:].rearrange("p b u q -> p b q u"),
+                )
+            codes = work.tile([P, SLAB], U32, name="y_codes", align_bytes=64)
+            scales = work.tile([P, SLAB], U8, name="y_scales", align_bytes=64)
+            nc.vector.quantize_mx(
+                out=codes[:].bitcast(FP8X4),
+                scales=scales[:],
+                in_=grouped[:].rearrange("p q t -> p (q t)"),
+            )
+            return codes, scales
+
+        def second_product(s, codes, scales):
+            for i in range(CHUNKS):
+                channels = slice(i * P, (i + 1) * P)
+                bank = out_banks.tile([P, SLAB], F32, name="out_bank")
+                nc.tensor.matmul_mx(
+                    out=bank[:],
+                    lhsT=out_words[:, channels].bitcast(FP8X4),
+                    lhsT_scale=out_plane[:, channels],
+                    rhs=codes[:].bitcast(FP8X4),
+                    rhs_scale=scales[:],
+                    start=True,
+                    stop=True,
+                )
+                result = sums.tile([P, SLAB], F32, name="result")
+                nc.scalar.activation(
+                    out=result[:], in_=bank[:], func=IDENTITY,
+                    bias=table[:, BIAS_COLUMN + i : BIAS_COLUMN + i + 1], scale=1.0,
+                )
+                nc.sync.dma_start(out=out_rows[i, :, s * SLAB : (s + 1) * SLAB], in_=result[:])
+
+        for s in range(SLABS + 1):
+            if s < SLABS:
+                x_codes, x_scales = quantise_x(s)
+                for j in range(CHUNKS):
+                    filters_d_and_w(s, j, x_codes, x_scales)
+            if s >= 1:
+                y3 = work.tile([P, CHUNKS, SLAB], BF16, name="y3")
+                for j in range(CHUNKS):
+                    filter_h(s - 1, j, y3)
+                y_codes, y_scales = quantise_y3(y3)
+                second_product(s - 1, y_codes, y_scales)

@@ -21,17 +21,22 @@ CHUNKS = CHANNELS // P
 H_PLANES, W_ROWS, D_COLS = 8, 16, 16
 PLANE = W_ROWS * D_COLS
 POSITIONS = H_PLANES * PLANE
-SLAB = 2 * PLANE
-SLABS = POSITIONS // SLAB
+GROUP = 2 * PLANE
+GROUPS = POSITIONS // GROUP
+SLABS = GROUPS + 1
+PADDED = D_COLS + PLANE + D_COLS
 TAPS = 3
 BIAS_COLUMN = 3 * TAPS * CHUNKS
 TABLE_COLUMNS = BIAS_COLUMN + CHUNKS
 
 FLOPS = 2 * 2 * CHANNELS * CHANNELS * POSITIONS + (3 * (2 * TAPS - 1) + 1) * CHANNELS * POSITIONS
 
-
 def tap_column(axis, k, j):
     return (axis * TAPS + k) * CHUNKS + j
+
+
+def slab_bounds(s):
+    return max(0, (2 * s - 1) * PLANE), min(POSITIONS, (2 * s + 1) * PLANE)
 
 
 def load_weight(nc, pool, words_dram, scales_dram, label):
@@ -58,26 +63,13 @@ def tile_lowrankconv3d_kernel(
     out_rows = out[0].rearrange("(i m) h w d -> i m (h w d)", m=P)
 
     with ExitStack() as ctx:
+        ctx.enter_context(tc.manual_schedule())
         keep = ctx.enter_context(tc.tile_pool(name="keep", bufs=1))
         work = ctx.enter_context(tc.tile_pool(name="work", bufs=2))
         sums = ctx.enter_context(tc.tile_pool(name="sums", bufs=4))
-        product_banks = ctx.enter_context(tc.psum_pool(name="product_banks", bufs=3))
+        product_banks = ctx.enter_context(tc.psum_pool(name="product_banks", bufs=4))
         turn_banks = ctx.enter_context(tc.psum_pool(name="turn_banks", bufs=3))
-        out_banks = ctx.enter_context(tc.psum_pool(name="out_banks", bufs=2))
-
-        x_raw = []
-        for s in range(SLABS):
-            x_raw.append(keep.tile([P, PACK, SLAB], BF16, name="x_raw%d" % s))
-        nc.sync.dma_start(out=x_raw[0][:], in_=x_rows[:, :, 0:SLAB])
-        in_words, in_plane = load_weight(nc, keep, U_c_in_words, U_c_in_scales, "u_in")
-        for s in range(1, SLABS):
-            nc.sync.dma_start(out=x_raw[s][:], in_=x_rows[:, :, s * SLAB : (s + 1) * SLAB])
-        out_words, out_plane = load_weight(nc, keep, U_c_out_words, U_c_out_scales, "u_out")
-
-        ident_bf16 = keep.tile([P, P], BF16, name="ident_bf16")
-        make_identity(nc, ident_bf16[:])
-        ident_f32 = keep.tile([P, P], F32, name="ident_f32")
-        make_identity(nc, ident_f32[:])
+        last_banks = ctx.enter_context(tc.psum_pool(name="last_banks", bufs=1))
 
         table_rows = keep.tile([P, P], BF16, name="table_rows")
         nc.vector.memset(table_rows[:], 0.0)
@@ -90,157 +82,318 @@ def tile_lowrankconv3d_kernel(
         nc.scalar.dma_start(
             out=table_rows[BIAS_COLUMN:TABLE_COLUMNS, :], in_=bias.rearrange("(i m) -> i m", m=P)
         )
-        table_bank = turn_banks.tile([P, P], BF16, tag="turn")
-        nc.tensor.transpose(table_bank[:], table_rows[:], ident_bf16[:])
+
+        x_raw = []
+        for s in range(SLABS):
+            lo, hi = slab_bounds(s)
+            x_raw.append(keep.tile([P, PACK, hi - lo], BF16, name="x_raw%d" % s))
+
+        def load_x(s):
+            lo, hi = slab_bounds(s)
+            nc.sync.dma_start(out=x_raw[s][:], in_=x_rows[:, :, lo:hi])
+
+        load_x(0)
+        in_words, in_plane = load_weight(nc, keep, U_c_in_words, U_c_in_scales, "u_in")
+        for s in range(1, SLABS):
+            load_x(s)
+        out_words, out_plane = load_weight(nc, keep, U_c_out_words, U_c_out_scales, "u_out")
+
+        ident_bf16 = keep.tile([P, P], BF16, name="ident_bf16")
+        make_identity(nc, ident_bf16[:])
+        ident_f32 = keep.tile([P, P], F32, name="ident_f32")
+        make_identity(nc, ident_f32[:])
+
         table = keep.tile([P, TABLE_COLUMNS], F32, name="table")
-        nc.vector.tensor_copy(out=table[:], in_=table_bank[:, 0:TABLE_COLUMNS])
+
+        def load_table():
+            table_bank = turn_banks.tile([P, P], BF16, tag="by_position")
+            nc.tensor.transpose(table_bank[:], table_rows[:], ident_bf16[:])
+            nc.vector.tensor_copy(out=table[:], in_=table_bank[:, 0:TABLE_COLUMNS])
 
         def tap(axis, k, j):
             column = tap_column(axis, k, j)
             return table[:, column : column + 1]
 
-        after_w = []
+        after_d = []
         for j in range(CHUNKS):
-            after_w.append(keep.tile([P, PLANE + POSITIONS], F32, name="after_w%d" % j))
-            nc.vector.memset(after_w[j][:, 0:PLANE], 0.0)
+            after_d.append(keep.tile([P, POSITIONS], F32, name="after_d%d" % j))
+        scaled = []
+        for parity in range(2):
+            scaled.append([])
+            for k in range(TAPS):
+                scaled[parity].append([])
+                for j in range(CHUNKS):
+                    padded = keep.tile([P, 2, PADDED], F32, name="scaled%d_%d_%d" % (parity, k, j))
+                    scaled[parity][k].append(padded)
+                    if k == 0:
+                        nc.gpsimd.memset(padded[:, :, 0:D_COLS], 0.0)
+                    if k == 2:
+                        nc.gpsimd.memset(padded[:, :, D_COLS + PLANE : PADDED], 0.0)
 
-        def quantise_x(s):
-            grouped = work.tile([P, SLAB, PACK], BF16, name="x_grouped", align_bytes=64)
-            source = x_raw[s][:].rearrange("p t (c i) -> p c t i", i=4)
-            target = grouped[:].rearrange("p (c i) t -> p c t i", i=4)
-            if s == 0:
+        x_grouped, x_codes, x_scales, y0, after_h = {}, {}, {}, {}, {}
+        by_position, pairs, by_word, y_grouped, y_codes, y_scales, out_bank = {}, {}, {}, {}, {}, {}, {}
+
+        PAIRS = ((0, 1), (2, 3))
+
+        def regroup_x(s, part, engine):
+            lo, hi = slab_bounds(s)
+            n = (hi - lo) // 2
+            if part == 0:
+                x_grouped[s] = keep.tile([P, GROUP, PACK], BF16, name="x_grouped%d" % s, align_bytes=64)
+            source = x_raw[s][:, :, part * n : (part + 1) * n].rearrange("p t (c i) -> p c t i", i=4)
+            target = x_grouped[s][:, part * n : (part + 1) * n, :].rearrange("p (c i) t -> p c t i", i=4)
+            if engine == "vector":
                 nc.vector.tensor_copy(out=target, in_=source)
             else:
                 nc.scalar.copy(out=target, in_=source)
-            codes = work.tile([P, SLAB], U32, name="x_codes", align_bytes=64)
-            scales = work.tile([P, SLAB], U8, name="x_scales", align_bytes=64)
-            nc.vector.quantize_mx(
-                out=codes[:].bitcast(FP8X4),
-                scales=scales[:],
-                in_=grouped[:].rearrange("p q t -> p (q t)"),
-            )
-            return codes, scales
 
-        def filters_d_and_w(s, j, codes, scales):
+        def quantise_x(s):
+            lo, hi = slab_bounds(s)
+            n = hi - lo
+            x_codes[s] = work.tile([P, GROUP], U32, name="x_codes", align_bytes=64)
+            x_scales[s] = work.tile([P, GROUP], U8, name="x_scales", align_bytes=64)
+            nc.vector.quantize_mx(
+                out=x_codes[s][:, 0:n].bitcast(FP8X4),
+                scales=x_scales[s][:, 0:n],
+                in_=x_grouped[s][:, 0:n, :].rearrange("p q t -> p (q t)"),
+            )
+
+        def first_product(s, j):
+            lo, hi = slab_bounds(s)
+            n = hi - lo
             ranks = slice(j * P, (j + 1) * P)
-            y0 = product_banks.tile([P, SLAB], F32, name="y0")
+            y0[s, j] = product_banks.tile([P, GROUP], F32, name="y0", tag="product")
             nc.tensor.matmul_mx(
-                out=y0[:],
+                out=y0[s, j][:, 0:n],
                 lhsT=in_words[:, ranks].bitcast(FP8X4),
                 lhsT_scale=in_plane[:, ranks],
-                rhs=codes[:].bitcast(FP8X4),
-                rhs_scale=scales[:],
+                rhs=x_codes[s][:, 0:n].bitcast(FP8X4),
+                rhs_scale=x_scales[s][:, 0:n],
                 start=True,
                 stop=True,
             )
-            after_d = sums.tile([P, SLAB], F32, name="after_d")
-            nc.scalar.activation(out=after_d[:], in_=y0[:], func=COPY, scale=tap(2, 1, j))
-            y0_rows = y0[:].rearrange("p (r d) -> p r d", d=D_COLS)
-            d_rows = after_d[:].rearrange("p (r d) -> p r d", d=D_COLS)
+
+        def d_middle(s, j):
+            lo, hi = slab_bounds(s)
+            nc.scalar.activation(out=after_d[j][:, lo:hi], in_=y0[s, j][:, 0 : hi - lo], func=COPY, scale=tap(2, 1, j))
+
+        def d_outer(s, j, k):
+            lo, hi = slab_bounds(s)
+            source = y0[s, j][:, 0 : hi - lo].rearrange("p (r d) -> p r d", d=D_COLS)
+            target = after_d[j][:, lo:hi].rearrange("p (r d) -> p r d", d=D_COLS)
+            if k == 0:
+                source, target = source[:, :, 0 : D_COLS - 1], target[:, :, 1:D_COLS]
+            else:
+                source, target = source[:, :, 1:D_COLS], target[:, :, 0 : D_COLS - 1]
             nc.vector.scalar_tensor_tensor(
-                out=d_rows[:, :, 1:D_COLS], in0=y0_rows[:, :, 0 : D_COLS - 1], scalar=tap(2, 0, j),
-                in1=d_rows[:, :, 1:D_COLS], op0=MULT, op1=ADD,
-            )
-            nc.vector.scalar_tensor_tensor(
-                out=d_rows[:, :, 0 : D_COLS - 1], in0=y0_rows[:, :, 1:D_COLS], scalar=tap(2, 2, j),
-                in1=d_rows[:, :, 0 : D_COLS - 1], op0=MULT, op1=ADD,
-            )
-            first = PLANE + s * SLAB
-            result = after_w[j][:, first : first + SLAB]
-            nc.scalar.activation(out=result, in_=after_d[:], func=COPY, scale=tap(1, 1, j))
-            d_planes = after_d[:].rearrange("p (h q) -> p h q", q=PLANE)
-            w_planes = result.rearrange("p (h q) -> p h q", q=PLANE)
-            nc.vector.scalar_tensor_tensor(
-                out=w_planes[:, :, D_COLS:PLANE], in0=d_planes[:, :, 0 : PLANE - D_COLS],
-                scalar=tap(1, 0, j), in1=w_planes[:, :, D_COLS:PLANE], op0=MULT, op1=ADD,
-            )
-            nc.vector.scalar_tensor_tensor(
-                out=w_planes[:, :, 0 : PLANE - D_COLS], in0=d_planes[:, :, D_COLS:PLANE],
-                scalar=tap(1, 2, j), in1=w_planes[:, :, 0 : PLANE - D_COLS], op0=MULT, op1=ADD,
+                out=target, in0=source, scalar=tap(2, k, j), in1=target, op0=MULT, op1=ADD
             )
 
-        def filter_h(s, j, y3):
-            first = PLANE + s * SLAB
-            volume = after_w[j]
-            partial = sums.tile([P, SLAB], F32, name="partial")
+        def h_middle(g, j):
+            after_h[g, j] = sums.tile([P, GROUP], F32, name="after_h")
             nc.scalar.activation(
-                out=partial[:], in_=volume[:, first - PLANE : first - PLANE + SLAB], func=COPY,
-                scale=tap(0, 0, j),
-            )
-            above = min(SLAB, POSITIONS - (s * SLAB + PLANE))
-            nc.vector.scalar_tensor_tensor(
-                out=partial[:, 0:above], in0=volume[:, first + PLANE : first + PLANE + above],
-                scalar=tap(0, 2, j), in1=partial[:, 0:above], op0=MULT, op1=ADD,
-            )
-            nc.vector.scalar_tensor_tensor(
-                out=y3[:, j, :], in0=volume[:, first : first + SLAB], scalar=tap(0, 1, j),
-                in1=partial[:], op0=MULT, op1=ADD,
+                out=after_h[g, j][:], in_=after_d[j][:, g * GROUP : (g + 1) * GROUP], func=COPY, scale=tap(0, 1, j)
             )
 
-        def quantise_y3(y3):
-            grouped = work.tile([P, SLAB, PACK], BF16, name="y_grouped", align_bytes=64)
+        def h_outer(g, j, k):
+            step = (k - 1) * PLANE
+            first = max(g * GROUP, -step)
+            last = min((g + 1) * GROUP, POSITIONS - step)
+            target = after_h[g, j][:, first - g * GROUP : last - g * GROUP]
+            nc.vector.scalar_tensor_tensor(
+                out=target, in0=after_d[j][:, first + step : last + step], scalar=tap(0, k, j), in1=target,
+                op0=MULT, op1=ADD,
+            )
+
+        def w_product(g, j, k):
+            target = scaled[g % 2][k][j][:, :, D_COLS : D_COLS + PLANE]
+            source = after_h[g, j][:].rearrange("p (h q) -> p h q", q=PLANE)
+            if k == 1 and j in PAIRS[0]:
+                nc.scalar.activation(out=target, in_=source, func=COPY, scale=tap(1, k, j))
+            else:
+                nc.vector.tensor_scalar_mul(out=target, in0=source, scalar1=tap(1, k, j))
+
+        def add_and_turn(g, b):
+            by_position[g, b] = turn_banks.tile([P, CHANNELS], F32, name="by_position")
+            plane, part = divmod(b * P, PLANE)
+            for j in range(CHUNKS):
+                for k in range(TAPS):
+                    first = part + k * D_COLS
+                    nc.tensor.matmul(
+                        out=by_position[g, b][:, j * P : (j + 1) * P],
+                        lhsT=scaled[g % 2][k][j][:, plane, first : first + P],
+                        rhs=ident_f32[:],
+                        start=(k == 0),
+                        stop=(k == TAPS - 1),
+                        is_transpose=True,
+                    )
+
+        def round_y3(g, b, engine):
+            pairs[g, b] = sums.tile([P, 2, 2 * P], BF16, name="pairs")
+            target = pairs[g, b][:].rearrange("q u (p e) -> q u p e", e=2)
+            source = by_position[g, b][:].rearrange("q (p u e) -> q u p e", u=2, e=2)
+            if engine == "vector":
+                nc.vector.tensor_copy(out=target, in_=source)
+            else:
+                nc.scalar.copy(out=target, in_=source)
+
+        def turn_back(g, b):
+            if b % 2 == 0:
+                by_word[g, b // 2] = last_banks.tile([P, 2, 2, P], F32, name="by_word")
+            for u in range(2):
+                nc.tensor.transpose(
+                    by_word[g, b // 2][:, b % 2, u, :], pairs[g, b][:, u, :].bitcast(F32), ident_f32[:]
+                )
+
+        def regroup_y3(g, half, engine):
+            if half == 0:
+                y_grouped[g] = work.tile([P, GROUP, PACK], BF16, name="y_grouped", align_bytes=64)
             grouped_pairs = (
-                grouped[:].rearrange("p q t -> p (q t)").bitcast(F32).rearrange("p (q u) -> p q u", u=2)
+                y_grouped[g][:].rearrange("p q t -> p (q t)").bitcast(F32).rearrange("p (q u) -> p q u", u=2)
             )
-            for half in range(SLAB // (2 * P)):
-                by_position = turn_banks.tile([P, 2, CHANNELS], BF16, tag="turn")
-                for b in range(2):
-                    q0 = (2 * half + b) * P
-                    for j in range(CHUNKS):
-                        nc.tensor.transpose(
-                            by_position[:, b, j * P : (j + 1) * P], y3[:, j, q0 : q0 + P], ident_bf16[:]
-                        )
-                pairs = work.tile([P, 2, 2, P], F32, name="pairs")
-                nc.scalar.copy(
-                    out=pairs[:], in_=by_position[:].bitcast(F32).rearrange("q b (p u) -> q b u p", u=2)
-                )
-                by_word = turn_banks.tile([P, 2, 2, P], F32, tag="turn")
-                for b in range(2):
-                    for u in range(2):
-                        nc.tensor.transpose(by_word[:, b, u, :], pairs[:, b, u, :], ident_f32[:])
-                nc.scalar.copy(
-                    out=grouped_pairs[:, 2 * half * P : 2 * (half + 1) * P, :].rearrange(
-                        "p (b q) u -> p b q u", b=2
-                    ),
-                    in_=by_word[:].rearrange("p b u q -> p b q u"),
-                )
-            codes = work.tile([P, SLAB], U32, name="y_codes", align_bytes=64)
-            scales = work.tile([P, SLAB], U8, name="y_scales", align_bytes=64)
+            target = grouped_pairs[:, 2 * half * P : 2 * (half + 1) * P, :].rearrange("p (b q) u -> p b q u", b=2)
+            source = by_word[g, half][:].rearrange("p b u q -> p b q u")
+            if engine == "vector":
+                nc.vector.tensor_copy(out=target, in_=source)
+            else:
+                nc.scalar.copy(out=target, in_=source)
+
+        def quantise_y3(g):
+            y_codes[g] = work.tile([P, GROUP], U32, name="y_codes", align_bytes=64)
+            y_scales[g] = work.tile([P, GROUP], U8, name="y_scales", align_bytes=64)
             nc.vector.quantize_mx(
-                out=codes[:].bitcast(FP8X4),
-                scales=scales[:],
-                in_=grouped[:].rearrange("p q t -> p (q t)"),
+                out=y_codes[g][:].bitcast(FP8X4),
+                scales=y_scales[g][:],
+                in_=y_grouped[g][:].rearrange("p q t -> p (q t)"),
             )
-            return codes, scales
 
-        def second_product(s, codes, scales):
-            for i in range(CHUNKS):
-                channels = slice(i * P, (i + 1) * P)
-                bank = out_banks.tile([P, SLAB], F32, name="out_bank")
-                nc.tensor.matmul_mx(
-                    out=bank[:],
-                    lhsT=out_words[:, channels].bitcast(FP8X4),
-                    lhsT_scale=out_plane[:, channels],
-                    rhs=codes[:].bitcast(FP8X4),
-                    rhs_scale=scales[:],
-                    start=True,
-                    stop=True,
-                )
-                result = sums.tile([P, SLAB], F32, name="result")
+        def second_product(g, i):
+            channels = slice(i * P, (i + 1) * P)
+            out_bank[g, i] = product_banks.tile([P, GROUP], F32, name="out_bank", tag="product")
+            nc.tensor.matmul_mx(
+                out=out_bank[g, i][:],
+                lhsT=out_words[:, channels].bitcast(FP8X4),
+                lhsT_scale=out_plane[:, channels],
+                rhs=y_codes[g][:].bitcast(FP8X4),
+                rhs_scale=y_scales[g][:],
+                start=True,
+                stop=True,
+            )
+
+        def finish(g, i, engine):
+            result = sums.tile([P, GROUP], F32, name="result")
+            bias_column = table[:, BIAS_COLUMN + i : BIAS_COLUMN + i + 1]
+            if engine == "vector":
+                nc.vector.tensor_scalar_add(out=result[:], in0=out_bank[g, i][:], scalar1=bias_column)
+            else:
                 nc.scalar.activation(
-                    out=result[:], in_=bank[:], func=IDENTITY,
-                    bias=table[:, BIAS_COLUMN + i : BIAS_COLUMN + i + 1], scale=1.0,
+                    out=result[:], in_=out_bank[g, i][:], func=IDENTITY, bias=bias_column, scale=1.0
                 )
-                nc.sync.dma_start(out=out_rows[i, :, s * SLAB : (s + 1) * SLAB], in_=result[:])
+            nc.sync.dma_start(out=out_rows[i, :, g * GROUP : (g + 1) * GROUP], in_=result[:])
 
-        for s in range(SLABS + 1):
-            if s < SLABS:
-                x_codes, x_scales = quantise_x(s)
-                for j in range(CHUNKS):
-                    filters_d_and_w(s, j, x_codes, x_scales)
-            if s >= 1:
-                y3 = work.tile([P, CHUNKS, SLAB], BF16, name="y3")
-                for j in range(CHUNKS):
-                    filter_h(s - 1, j, y3)
-                y_codes, y_scales = quantise_y3(y3)
-                second_product(s - 1, y_codes, y_scales)
+        def is_slab(s):
+            return 0 <= s < SLABS
+
+        def is_group(g):
+            return 0 <= g < GROUPS
+
+        regroup_x(0, 0, "vector")
+        regroup_x(0, 1, "scalar")
+        quantise_x(0)
+        load_table()
+        for j in range(CHUNKS):
+            first_product(0, j)
+        regroup_x(1, 0, "vector")
+        regroup_x(1, 1, "vector")
+        quantise_x(1)
+        for j in PAIRS[0]:
+            d_middle(0, j)
+
+        for s in range(SLABS + 2):
+            g = s - 1
+            c = s - 2
+            f = s - 3
+            helper = "vector" if s >= SLABS else "scalar"
+            if is_group(f):
+                quantise_y3(f)
+            if is_group(c):
+                add_and_turn(c, 0)
+                add_and_turn(c, 1)
+            if is_slab(s):
+                for k in (0, 2):
+                    for j in PAIRS[0]:
+                        d_outer(s, j, k)
+                for j in PAIRS[1]:
+                    d_middle(s, j)
+            if is_slab(s + 2) and s > 0:
+                regroup_x(s + 2, 0, "scalar")
+            if is_slab(s):
+                for k in (0, 2):
+                    for j in PAIRS[1]:
+                        d_outer(s, j, k)
+            if s == 0:
+                regroup_x(2, 0, "vector")
+                regroup_x(2, 1, "vector")
+            if is_slab(s + 1) and s > 0:
+                quantise_x(s + 1)
+            if is_group(g):
+                for j in PAIRS[0]:
+                    h_middle(g, j)
+            if is_group(f):
+                second_product(f, 0)
+                second_product(f, 1)
+            if is_group(c):
+                round_y3(c, 0, "scalar")
+                round_y3(c, 1, helper)
+            if is_group(g):
+                for k in (0, 2):
+                    for j in PAIRS[0]:
+                        h_outer(g, j, k)
+                for j in PAIRS[1]:
+                    h_middle(g, j)
+            if is_group(c):
+                turn_back(c, 0)
+                turn_back(c, 1)
+                add_and_turn(c, 2)
+                add_and_turn(c, 3)
+            if is_group(f):
+                finish(f, 0, "scalar")
+                finish(f, 1, helper)
+            if is_group(g):
+                for k in (0, 2):
+                    for j in PAIRS[1]:
+                        h_outer(g, j, k)
+            if is_group(f):
+                second_product(f, 2)
+                second_product(f, 3)
+            if is_slab(s + 1):
+                for j in PAIRS[0]:
+                    first_product(s + 1, j)
+            if is_group(c):
+                regroup_y3(c, 0, helper)
+                round_y3(c, 2, "scalar")
+                round_y3(c, 3, helper)
+            if is_group(g):
+                for j in PAIRS[0]:
+                    for k in range(TAPS):
+                        w_product(g, j, k)
+            if is_group(c):
+                turn_back(c, 2)
+                turn_back(c, 3)
+            if is_group(f):
+                finish(f, 2, "scalar")
+                finish(f, 3, helper)
+            if is_slab(s + 1):
+                for j in PAIRS[0]:
+                    d_middle(s + 1, j)
+            if is_group(g):
+                for j in PAIRS[1]:
+                    for k in range(TAPS):
+                        w_product(g, j, k)
+            if is_slab(s + 1):
+                for j in PAIRS[1]:
+                    first_product(s + 1, j)
+            if is_group(c):
+                regroup_y3(c, 1, "scalar")
+            if is_slab(s + 2) and s > 0:
+                regroup_x(s + 2, 1, "scalar")

@@ -208,7 +208,7 @@ def tile_lowrankconv3d_kernel(
         def w_product(g, j, k):
             target = scaled[g % 2][k][j][:, :, D_COLS : D_COLS + PLANE]
             source = after_h[g, j][:].rearrange("p (h q) -> p h q", q=PLANE)
-            if k == 1 and j in PAIRS[0]:
+            if k == 1 and (j in PAIRS[0] or g < GROUPS // 2):
                 nc.scalar.activation(out=target, in_=source, func=COPY, scale=tap(1, k, j))
             else:
                 nc.vector.tensor_scalar_mul(out=target, in0=source, scalar1=tap(1, k, j))
@@ -332,8 +332,8 @@ def tile_lowrankconv3d_kernel(
                     for j in PAIRS[1]:
                         d_outer(s, j, k)
             if s == 0:
-                regroup_x(2, 0, "vector")
-                regroup_x(2, 1, "vector")
+                regroup_x(2, 0, "scalar")
+                regroup_x(2, 1, "scalar")
             if is_slab(s + 1) and s > 0:
                 quantise_x(s + 1)
             if is_group(g):

@@ -24,7 +24,7 @@ POSITIONS = H_PLANES * PLANE
 GROUP = 2 * PLANE
 GROUPS = POSITIONS // GROUP
 SLABS = GROUPS + 1
-PADDED = D_COLS + PLANE + D_COLS
+ROWS = GROUP // D_COLS
 TAPS = 3
 BIAS_COLUMN = 3 * TAPS * CHUNKS
 TABLE_COLUMNS = BIAS_COLUMN + CHUNKS
@@ -123,12 +123,12 @@ def tile_lowrankconv3d_kernel(
             for k in range(TAPS):
                 scaled[parity].append([])
                 for j in range(CHUNKS):
-                    padded = keep.tile([P, 2, PADDED], F32, name="scaled%d_%d_%d" % (parity, k, j))
+                    padded = keep.tile([P, ROWS + 1, D_COLS], F32, name="scaled%d_%d_%d" % (parity, k, j))
                     scaled[parity][k].append(padded)
                     if k == 0:
-                        nc.gpsimd.memset(padded[:, :, 0:D_COLS], 0.0)
+                        nc.vector.memset(padded[:, :, D_COLS - 1 : D_COLS], 0.0)
                     if k == 2:
-                        nc.gpsimd.memset(padded[:, :, D_COLS + PLANE : PADDED], 0.0)
+                        nc.vector.memset(padded[:, :, 0:1], 0.0)
 
         x_grouped, x_codes, x_scales, y0, after_h = {}, {}, {}, {}, {}
         by_position, pairs, by_word, y_grouped, y_codes, y_scales, out_bank = {}, {}, {}, {}, {}, {}, {}
@@ -175,18 +175,18 @@ def tile_lowrankconv3d_kernel(
 
         def d_middle(s, j):
             lo, hi = slab_bounds(s)
-            nc.scalar.activation(out=after_d[j][:, lo:hi], in_=y0[s, j][:, 0 : hi - lo], func=COPY, scale=tap(2, 1, j))
+            nc.scalar.activation(out=after_d[j][:, lo:hi], in_=y0[s, j][:, 0 : hi - lo], func=COPY, scale=tap(1, 1, j))
 
         def d_outer(s, j, k):
             lo, hi = slab_bounds(s)
-            source = y0[s, j][:, 0 : hi - lo].rearrange("p (r d) -> p r d", d=D_COLS)
-            target = after_d[j][:, lo:hi].rearrange("p (r d) -> p r d", d=D_COLS)
+            source = y0[s, j][:, 0 : hi - lo].rearrange("p (h q) -> p h q", q=PLANE)
+            target = after_d[j][:, lo:hi].rearrange("p (h q) -> p h q", q=PLANE)
             if k == 0:
-                source, target = source[:, :, 0 : D_COLS - 1], target[:, :, 1:D_COLS]
+                source, target = source[:, :, 0 : PLANE - D_COLS], target[:, :, D_COLS:PLANE]
             else:
-                source, target = source[:, :, 1:D_COLS], target[:, :, 0 : D_COLS - 1]
+                source, target = source[:, :, D_COLS:PLANE], target[:, :, 0 : PLANE - D_COLS]
             nc.vector.scalar_tensor_tensor(
-                out=target, in0=source, scalar=tap(2, k, j), in1=target, op0=MULT, op1=ADD
+                out=target, in0=source, scalar=tap(1, k, j), in1=target, op0=MULT, op1=ADD
             )
 
         def h_middle(g, j):
@@ -206,22 +206,23 @@ def tile_lowrankconv3d_kernel(
             )
 
         def w_product(g, j, k):
-            target = scaled[g % 2][k][j][:, :, D_COLS : D_COLS + PLANE]
-            source = after_h[g, j][:].rearrange("p (h q) -> p h q", q=PLANE)
+            columns = (slice(0, D_COLS - 1), slice(0, D_COLS), slice(1, D_COLS))[k]
+            first_row = 1 if k == 0 else 0
+            target = scaled[g % 2][k][j][:, first_row : first_row + ROWS, columns]
+            source = after_h[g, j][:].rearrange("p (r d) -> p r d", d=D_COLS)[:, :, columns]
             if k == 1 and (j in PAIRS[0] or g < GROUPS // 2):
-                nc.scalar.activation(out=target, in_=source, func=COPY, scale=tap(1, k, j))
+                nc.scalar.activation(out=target, in_=source, func=COPY, scale=tap(2, k, j))
             else:
-                nc.vector.tensor_scalar_mul(out=target, in0=source, scalar1=tap(1, k, j))
+                nc.vector.tensor_scalar_mul(out=target, in0=source, scalar1=tap(2, k, j))
 
         def add_and_turn(g, b):
             by_position[g, b] = turn_banks.tile([P, CHANNELS], F32, name="by_position")
-            plane, part = divmod(b * P, PLANE)
             for j in range(CHUNKS):
                 for k in range(TAPS):
-                    first = part + k * D_COLS
+                    first = (D_COLS if k == 0 else 0) + b * P + k - 1
                     nc.tensor.matmul(
                         out=by_position[g, b][:, j * P : (j + 1) * P],
-                        lhsT=scaled[g % 2][k][j][:, plane, first : first + P],
+                        lhsT=scaled[g % 2][k][j][:].rearrange("p r d -> p (r d)")[:, first : first + P],
                         rhs=ident_f32[:],
                         start=(k == 0),
                         stop=(k == TAPS - 1),

@@ -126,9 +126,9 @@ def tile_lowrankconv3d_kernel(
                     padded = keep.tile([P, ROWS + 1, D_COLS], F32, name="scaled%d_%d_%d" % (parity, k, j))
                     scaled[parity][k].append(padded)
                     if k == 0:
-                        nc.vector.memset(padded[:, :, D_COLS - 1 : D_COLS], 0.0)
+                        nc.gpsimd.memset(padded[:, :, D_COLS - 4 : D_COLS], 0.0)
                     if k == 2:
-                        nc.vector.memset(padded[:, :, 0:1], 0.0)
+                        nc.gpsimd.memset(padded[:, :, 0:4], 0.0)
 
         x_grouped, x_codes, x_scales, y0, after_h = {}, {}, {}, {}, {}
         by_position, pairs, by_word, y_grouped, y_codes, y_scales, out_bank = {}, {}, {}, {}, {}, {}, {}

@@ -123,12 +123,12 @@ def tile_lowrankconv3d_kernel(
             for k in range(TAPS):
                 scaled[parity].append([])
                 for j in range(CHUNKS):
-                    padded = keep.tile([P, ROWS + 1, D_COLS], F32, name="scaled%d_%d_%d" % (parity, k, j))
+                    padded = keep.tile([P, ROWS, D_COLS], F32, name="scaled%d_%d_%d" % (parity, k, j))
                     scaled[parity][k].append(padded)
                     if k == 0:
-                        nc.gpsimd.memset(padded[:, :, D_COLS - 4 : D_COLS], 0.0)
-                    if k == 2:
                         nc.gpsimd.memset(padded[:, :, 0:4], 0.0)
+                    if k == 2:
+                        nc.gpsimd.memset(padded[:, :, D_COLS - 4 : D_COLS], 0.0)
 
         x_grouped, x_codes, x_scales, y0, after_h = {}, {}, {}, {}, {}
         by_position, pairs, by_word, y_grouped, y_codes, y_scales, out_bank = {}, {}, {}, {}, {}, {}, {}
@@ -144,6 +144,8 @@ def tile_lowrankconv3d_kernel(
             target = x_grouped[s][:, part * n : (part + 1) * n, :].rearrange("p (c i) t -> p c t i", i=4)
             if engine == "vector":
                 nc.vector.tensor_copy(out=target, in_=source)
+            elif engine == "gpsimd":
+                nc.gpsimd.tensor_scalar(out=target, in0=source, scalar1=1.0, scalar2=0.0, op0=MULT, op1=ADD)
             else:
                 nc.scalar.copy(out=target, in_=source)
 
@@ -206,10 +208,10 @@ def tile_lowrankconv3d_kernel(
             )
 
         def w_product(g, j, k):
-            columns = (slice(0, D_COLS - 1), slice(0, D_COLS), slice(1, D_COLS))[k]
-            first_row = 1 if k == 0 else 0
-            target = scaled[g % 2][k][j][:, first_row : first_row + ROWS, columns]
-            source = after_h[g, j][:].rearrange("p (r d) -> p r d", d=D_COLS)[:, :, columns]
+            taken = (slice(0, D_COLS - 1), slice(0, D_COLS), slice(1, D_COLS))[k]
+            put = (slice(1, D_COLS), slice(0, D_COLS), slice(0, D_COLS - 1))[k]
+            target = scaled[g % 2][k][j][:, :, put]
+            source = after_h[g, j][:].rearrange("p (r d) -> p r d", d=D_COLS)[:, :, taken]
             if k == 1 and (j in PAIRS[0] or g < GROUPS // 2):
                 nc.scalar.activation(out=target, in_=source, func=COPY, scale=tap(2, k, j))
             else:
@@ -219,10 +221,9 @@ def tile_lowrankconv3d_kernel(
             by_position[g, b] = turn_banks.tile([P, CHANNELS], F32, name="by_position")
             for j in range(CHUNKS):
                 for k in range(TAPS):
-                    first = (D_COLS if k == 0 else 0) + b * P + k - 1
                     nc.tensor.matmul(
                         out=by_position[g, b][:, j * P : (j + 1) * P],
-                        lhsT=scaled[g % 2][k][j][:].rearrange("p r d -> p (r d)")[:, first : first + P],
+                        lhsT=scaled[g % 2][k][j][:].rearrange("p r d -> p (r d)")[:, b * P : (b + 1) * P],
                         rhs=ident_f32[:],
                         start=(k == 0),
                         stop=(k == TAPS - 1),
@@ -327,7 +328,7 @@ def tile_lowrankconv3d_kernel(
                 for j in PAIRS[1]:
                     d_middle(s, j)
             if is_slab(s + 2) and s > 0:
-                regroup_x(s + 2, 0, "scalar")
+                regroup_x(s + 2, 0, "gpsimd")
             if is_slab(s):
                 for k in (0, 2):
                     for j in PAIRS[1]:
@@ -397,4 +398,4 @@ def tile_lowrankconv3d_kernel(
             if is_group(c):
                 regroup_y3(c, 1, "scalar")
             if is_slab(s + 2) and s > 0:
-                regroup_x(s + 2, 1, "scalar")
+                regroup_x(s + 2, 1, "gpsimd")

@@ -193,9 +193,15 @@ def tile_lowrankconv3d_kernel(
 
         def h_middle(g, j):
             after_h[g, j] = sums.tile([P, GROUP], F32, name="after_h")
-            nc.scalar.activation(
-                out=after_h[g, j][:], in_=after_d[j][:, g * GROUP : (g + 1) * GROUP], func=COPY, scale=tap(0, 1, j)
-            )
+            if j in PAIRS[0]:
+                nc.gpsimd.tensor_scalar(
+                    out=after_h[g, j][:], in0=after_d[j][:, g * GROUP : (g + 1) * GROUP], scalar1=tap(0, 1, j), scalar2=0.0,
+                    op0=MULT, op1=ADD,
+                )
+            else:
+                nc.scalar.activation(
+                    out=after_h[g, j][:], in_=after_d[j][:, g * GROUP : (g + 1) * GROUP], func=COPY, scale=tap(0, 1, j)
+                )
 
         def h_outer(g, j, k):
             step = (k - 1) * PLANE

@@ -26,6 +26,7 @@ GROUPS = POSITIONS // GROUP
 SLABS = GROUPS + 1
 ROWS = GROUP // D_COLS
 TAPS = 3
+DIAGONAL_CHUNKS = (0, 1, 2)
 BIAS_COLUMN = 3 * TAPS * CHUNKS
 TABLE_COLUMNS = BIAS_COLUMN + CHUNKS
 
@@ -114,6 +115,16 @@ def tile_lowrankconv3d_kernel(
             column = tap_column(axis, k, j)
             return table[:, column : column + 1]
 
+        diagonal = {}
+        for j in DIAGONAL_CHUNKS:
+            diagonal[j] = keep.tile([P, P], F32, name="diagonal%d" % j)
+
+        def fill_diagonals():
+            for j in DIAGONAL_CHUNKS:
+                nc.gpsimd.tensor_scalar(
+                    out=diagonal[j][:], in0=ident_f32[:], scalar1=tap(2, 1, j), scalar2=0.0, op0=MULT, op1=ADD
+                )
+
         after_d = []
         for j in range(CHUNKS):
             after_d.append(keep.tile([P, POSITIONS], F32, name="after_d%d" % j))
@@ -192,7 +203,7 @@ def tile_lowrankconv3d_kernel(
             )
 
         def h_middle(g, j):
-            after_h[g, j] = sums.tile([P, GROUP], F32, name="after_h")
+            after_h[g, j] = sums.tile([P, GROUP], F32, name="after_h", bufs=8)
             if j in PAIRS[0]:
                 nc.gpsimd.tensor_scalar(
                     out=after_h[g, j][:], in0=after_d[j][:, g * GROUP : (g + 1) * GROUP], scalar1=tap(0, 1, j), scalar2=0.0,
@@ -216,9 +227,11 @@ def tile_lowrankconv3d_kernel(
         def w_product(g, j, k):
             taken = (slice(0, D_COLS - 1), slice(0, D_COLS), slice(1, D_COLS))[k]
             put = (slice(1, D_COLS), slice(0, D_COLS), slice(0, D_COLS - 1))[k]
+            if k == 1 and j in DIAGONAL_CHUNKS:
+                return
             target = scaled[g % 2][k][j][:, :, put]
             source = after_h[g, j][:].rearrange("p (r d) -> p r d", d=D_COLS)[:, :, taken]
-            if k == 1 and (j in PAIRS[0] or g < GROUPS // 2):
+            if k == 1:
                 nc.scalar.activation(out=target, in_=source, func=COPY, scale=tap(2, k, j))
             else:
                 nc.vector.tensor_scalar_mul(out=target, in0=source, scalar1=tap(2, k, j))
@@ -227,13 +240,17 @@ def tile_lowrankconv3d_kernel(
             by_position[g, b] = turn_banks.tile([P, CHANNELS], F32, name="by_position")
             for j in range(CHUNKS):
                 for k in range(TAPS):
+                    if k == 1 and j in DIAGONAL_CHUNKS:
+                        source, factor = after_h[g, j][:], diagonal[j]
+                    else:
+                        source, factor = scaled[g % 2][k][j][:].rearrange("p r d -> p (r d)"), ident_f32
                     nc.tensor.matmul(
                         out=by_position[g, b][:, j * P : (j + 1) * P],
-                        lhsT=scaled[g % 2][k][j][:].rearrange("p r d -> p (r d)")[:, b * P : (b + 1) * P],
-                        rhs=ident_f32[:],
+                        lhsT=source[:, b * P : (b + 1) * P],
+                        rhs=factor[:],
                         start=(k == 0),
                         stop=(k == TAPS - 1),
-                        is_transpose=True,
+                        is_transpose=factor is ident_f32,
                     )
 
         def round_y3(g, b, engine):
@@ -309,6 +326,7 @@ def tile_lowrankconv3d_kernel(
         regroup_x(0, 1, "scalar")
         quantise_x(0)
         load_table()
+        fill_diagonals()
         for j in range(CHUNKS):
             first_product(0, j)
         regroup_x(1, 0, "vector")

@@ -26,22 +26,17 @@ GROUPS = POSITIONS // GROUP
 SLABS = GROUPS + 1
 ROWS = GROUP // D_COLS
 TAPS = 3
-DIAGONAL_CHUNKS = (0, 1, 2)
-BIAS_COLUMN = 3 * TAPS * CHUNKS
-TABLE_COLUMNS = BIAS_COLUMN + CHUNKS
+GAP = 8
+PADDED_ROW = GAP + D_COLS
+W_AXIS, H_AXIS, D_AXIS = 0, 1, 2
 
 FLOPS = 2 * 2 * CHANNELS * CHANNELS * POSITIONS + (3 * (2 * TAPS - 1) + 1) * CHANNELS * POSITIONS
-
-def tap_column(axis, k, j):
-    return (axis * TAPS + k) * CHUNKS + j
-
 
 def slab_bounds(s):
     return max(0, (2 * s - 1) * PLANE), min(POSITIONS, (2 * s + 1) * PLANE)
 
 
-def load_weight(nc, pool, words_dram, scales_dram, label):
-    words = pool.tile([P, CHANNELS], U32, name=label + "_words", align_bytes=64)
+def load_scales(nc, pool, scales_dram, label):
     plane = pool.tile([P, CHANNELS], U8, name=label + "_plane", align_bytes=64)
     nc.vector.memset(plane[:].bitcast(I32), 0)
     for quadrant in range(4):
@@ -49,11 +44,16 @@ def load_weight(nc, pool, words_dram, scales_dram, label):
             out=plane[32 * quadrant : 32 * quadrant + 4, :].bitcast(I32),
             in_=scales_dram[0, 4 * quadrant : 4 * quadrant + 4, :].bitcast(I32),
         )
+    return plane
+
+
+def load_words(nc, pool, words_dram, label):
+    words = pool.tile([P, CHANNELS], U32, name=label + "_words", align_bytes=64)
     nc.sync.dma_start(
         out=words[:].bitcast(I32),
         in_=words_dram[0].rearrange("p n t -> p (n t)").bitcast(I32),
     )
-    return words, plane
+    return words
 
 
 def tile_lowrankconv3d_kernel(
@@ -72,18 +72,6 @@ def tile_lowrankconv3d_kernel(
         turn_banks = ctx.enter_context(tc.psum_pool(name="turn_banks", bufs=3))
         last_banks = ctx.enter_context(tc.psum_pool(name="last_banks", bufs=1))
 
-        table_rows = keep.tile([P, P], BF16, name="table_rows")
-        nc.vector.memset(table_rows[:], 0.0)
-        for axis, taps in enumerate((U_kh, U_kw, U_kd)):
-            first = tap_column(axis, 0, 0)
-            nc.scalar.dma_start(
-                out=table_rows[first : first + TAPS * CHUNKS, :],
-                in_=taps.rearrange("k (j m) -> (k j) m", m=P),
-            )
-        nc.scalar.dma_start(
-            out=table_rows[BIAS_COLUMN:TABLE_COLUMNS, :], in_=bias.rearrange("(i m) -> i m", m=P)
-        )
-
         x_raw = []
         for s in range(SLABS):
             lo, hi = slab_bounds(s)
@@ -93,36 +81,54 @@ def tile_lowrankconv3d_kernel(
             lo, hi = slab_bounds(s)
             nc.sync.dma_start(out=x_raw[s][:], in_=x_rows[:, :, lo:hi])
 
+        tap_rows = keep.tile([P, 3, 16], BF16, name="tap_rows")
+        for axis, taps in enumerate((U_kw, U_kh, U_kd)):
+            nc.scalar.dma_start(
+                out=tap_rows[:, axis, 0 : TAPS * PACK].rearrange("p (k t) -> p k t", t=PACK),
+                in_=taps.rearrange("k (p t) -> p k t", t=PACK),
+            )
+        bias_rows = keep.tile([P, CHUNKS], BF16, name="bias_rows")
+        nc.scalar.dma_start(out=bias_rows[:], in_=bias.rearrange("(i m) -> m i", m=P))
+
         load_x(0)
-        in_words, in_plane = load_weight(nc, keep, U_c_in_words, U_c_in_scales, "u_in")
+        in_plane = load_scales(nc, keep, U_c_in_scales, "u_in")
+        in_words = load_words(nc, keep, U_c_in_words, "u_in")
         for s in range(1, SLABS):
             load_x(s)
-        out_words, out_plane = load_weight(nc, keep, U_c_out_words, U_c_out_scales, "u_out")
+        out_plane = load_scales(nc, keep, U_c_out_scales, "u_out")
+        out_words = load_words(nc, keep, U_c_out_words, "u_out")
 
-        ident_bf16 = keep.tile([P, P], BF16, name="ident_bf16")
-        make_identity(nc, ident_bf16[:])
         ident_f32 = keep.tile([P, P], F32, name="ident_f32")
         make_identity(nc, ident_f32[:])
 
-        table = keep.tile([P, TABLE_COLUMNS], F32, name="table")
+        sorted_words = keep.tile([P, CHUNKS, P], U32, name="sorted_words", align_bytes=64)
+        sorted_plane = keep.tile([P, CHUNKS, P], U8, name="sorted_plane", align_bytes=64)
 
-        def load_table():
-            table_bank = turn_banks.tile([P, P], BF16, tag="by_position")
-            nc.tensor.transpose(table_bank[:], table_rows[:], ident_bf16[:])
-            nc.vector.tensor_copy(out=table[:], in_=table_bank[:, 0:TABLE_COLUMNS])
+        def sort_u_in(p):
+            chunks = slice(2 * p, 2 * p + 2)
+            nc.vector.tensor_copy(
+                out=sorted_words[:, chunks, :].bitcast(I32),
+                in_=in_words[:].bitcast(I32).rearrange("p (m t) -> p t m", t=CHUNKS)[:, chunks, :],
+            )
+            nc.vector.tensor_copy(
+                out=sorted_plane[:, chunks, :], in_=in_plane[:].rearrange("p (m t) -> p t m", t=CHUNKS)[:, chunks, :]
+            )
 
-        def tap(axis, k, j):
-            column = tap_column(axis, k, j)
-            return table[:, column : column + 1]
+        table = keep.tile([P, 3, TAPS * PACK], F32, name="table")
+        bias_table = keep.tile([P, CHUNKS], F32, name="bias_table")
+
+        def tap(axis, k, t):
+            column = k * PACK + t
+            return table[:, axis, column : column + 1]
 
         diagonal = {}
-        for j in DIAGONAL_CHUNKS:
+        for j in range(CHUNKS):
             diagonal[j] = keep.tile([P, P], F32, name="diagonal%d" % j)
 
         def fill_diagonals():
-            for j in DIAGONAL_CHUNKS:
+            for j in range(CHUNKS):
                 nc.gpsimd.tensor_scalar(
-                    out=diagonal[j][:], in0=ident_f32[:], scalar1=tap(2, 1, j), scalar2=0.0, op0=MULT, op1=ADD
+                    out=diagonal[j][:], in0=ident_f32[:], scalar1=tap(D_AXIS, 1, j), scalar2=0.0, op0=MULT, op1=ADD
                 )
 
         after_d = []
@@ -141,8 +147,52 @@ def tile_lowrankconv3d_kernel(
                     if k == 2:
                         nc.gpsimd.memset(padded[:, :, D_COLS - 4 : D_COLS], 0.0)
 
+        LAST = GROUPS - 1
+        padded_rows = []
+        for j in range(CHUNKS):
+            padded = keep.tile([P, ROWS + 1, PADDED_ROW], F32, name="padded%d" % j)
+            nc.gpsimd.memset(padded[:, :, 0:GAP], 0.0)
+            padded_rows.append(padded)
+        y3 = keep.tile([P, CHUNKS, GROUP], BF16, name="y3")
+
+        def last_rows(j, shift):
+            first = GAP + shift
+            flat = padded_rows[j][:].rearrange("p r c -> p (r c)")[:, first : first + ROWS * PADDED_ROW]
+            return flat.rearrange("p (r c) -> p r c", c=PADDED_ROW)[:, :, 0:D_COLS]
+
+        def rows_after_h(g, j):
+            if g == LAST:
+                return last_rows(j, 0)
+            return after_h[g, j][:].rearrange("p (r d) -> p r d", d=D_COLS)
+
+        def copy(engine, target, source):
+            if engine == "vector":
+                nc.vector.tensor_copy(out=target, in_=source)
+            elif engine == "gpsimd":
+                nc.gpsimd.tensor_scalar(out=target, in0=source, scalar1=1.0, scalar2=0.0, op0=MULT, op1=ADD)
+            else:
+                nc.scalar.copy(out=target, in_=source)
+
+        def times_tap(engine, target, source, factor):
+            if engine == "gpsimd":
+                nc.gpsimd.tensor_scalar(out=target, in0=source, scalar1=factor, scalar2=0.0, op0=MULT, op1=ADD)
+            elif engine == "vector":
+                nc.vector.tensor_scalar_mul(out=target, in0=source, scalar1=factor)
+            else:
+                nc.scalar.activation(out=target, in_=source, func=COPY, scale=factor)
+
+        def add_tap(target, source, factor, total):
+            nc.vector.scalar_tensor_tensor(out=target, in0=source, scalar=factor, in1=total, op0=MULT, op1=ADD)
+
+        def side_by_side(engine, grouped, rows, lo, hi):
+            copy(
+                engine,
+                grouped[:, lo:hi, :].rearrange("p (c i) t -> p c t i", i=4),
+                rows[:, :, lo:hi].rearrange("p t (c i) -> p c t i", i=4),
+            )
+
         x_grouped, x_codes, x_scales, y0, after_h = {}, {}, {}, {}, {}
-        by_position, pairs, by_word, y_grouped, y_codes, y_scales, out_bank = {}, {}, {}, {}, {}, {}, {}
+        d_sum, by_position, pairs, by_word, y_grouped, y_codes, y_scales, out_bank = {}, {}, {}, {}, {}, {}, {}, {}
 
         PAIRS = ((0, 1), (2, 3))
 
@@ -151,14 +201,7 @@ def tile_lowrankconv3d_kernel(
             n = (hi - lo) // 2
             if part == 0:
                 x_grouped[s] = keep.tile([P, GROUP, PACK], BF16, name="x_grouped%d" % s, align_bytes=64)
-            source = x_raw[s][:, :, part * n : (part + 1) * n].rearrange("p t (c i) -> p c t i", i=4)
-            target = x_grouped[s][:, part * n : (part + 1) * n, :].rearrange("p (c i) t -> p c t i", i=4)
-            if engine == "vector":
-                nc.vector.tensor_copy(out=target, in_=source)
-            elif engine == "gpsimd":
-                nc.gpsimd.tensor_scalar(out=target, in0=source, scalar1=1.0, scalar2=0.0, op0=MULT, op1=ADD)
-            else:
-                nc.scalar.copy(out=target, in_=source)
+            side_by_side(engine, x_grouped[s], x_raw[s], part * n, (part + 1) * n)
 
         def quantise_x(s):
             lo, hi = slab_bounds(s)
@@ -174,12 +217,11 @@ def tile_lowrankconv3d_kernel(
         def first_product(s, j):
             lo, hi = slab_bounds(s)
             n = hi - lo
-            ranks = slice(j * P, (j + 1) * P)
             y0[s, j] = product_banks.tile([P, GROUP], F32, name="y0", tag="product")
             nc.tensor.matmul_mx(
                 out=y0[s, j][:, 0:n],
-                lhsT=in_words[:, ranks].bitcast(FP8X4),
-                lhsT_scale=in_plane[:, ranks],
+                lhsT=sorted_words[:, j, :].bitcast(FP8X4),
+                lhsT_scale=sorted_plane[:, j, :],
                 rhs=x_codes[s][:, 0:n].bitcast(FP8X4),
                 rhs_scale=x_scales[s][:, 0:n],
                 start=True,
@@ -188,7 +230,7 @@ def tile_lowrankconv3d_kernel(
 
         def d_middle(s, j):
             lo, hi = slab_bounds(s)
-            nc.scalar.activation(out=after_d[j][:, lo:hi], in_=y0[s, j][:, 0 : hi - lo], func=COPY, scale=tap(1, 1, j))
+            nc.scalar.activation(out=after_d[j][:, lo:hi], in_=y0[s, j][:, 0 : hi - lo], func=COPY, scale=tap(W_AXIS, 1, j))
 
         def d_outer(s, j, k):
             lo, hi = slab_bounds(s)
@@ -199,48 +241,57 @@ def tile_lowrankconv3d_kernel(
             else:
                 source, target = source[:, :, D_COLS:PLANE], target[:, :, 0 : PLANE - D_COLS]
             nc.vector.scalar_tensor_tensor(
-                out=target, in0=source, scalar=tap(1, k, j), in1=target, op0=MULT, op1=ADD
+                out=target, in0=source, scalar=tap(W_AXIS, k, j), in1=target, op0=MULT, op1=ADD
             )
 
         def h_middle(g, j):
-            after_h[g, j] = sums.tile([P, GROUP], F32, name="after_h", bufs=8)
-            if j in PAIRS[0]:
-                nc.gpsimd.tensor_scalar(
-                    out=after_h[g, j][:], in0=after_d[j][:, g * GROUP : (g + 1) * GROUP], scalar1=tap(0, 1, j), scalar2=0.0,
-                    op0=MULT, op1=ADD,
-                )
-            else:
-                nc.scalar.activation(
-                    out=after_h[g, j][:], in_=after_d[j][:, g * GROUP : (g + 1) * GROUP], func=COPY, scale=tap(0, 1, j)
-                )
+            if g < LAST:
+                after_h[g, j] = sums.tile([P, GROUP], F32, name="after_h", bufs=8)
+            source = after_d[j][:, g * GROUP : (g + 1) * GROUP].rearrange("p (r d) -> p r d", d=D_COLS)
+            times_tap("gpsimd" if j in PAIRS[0] else "scalar", rows_after_h(g, j), source, tap(H_AXIS, 1, j))
 
         def h_outer(g, j, k):
             step = (k - 1) * PLANE
             first = max(g * GROUP, -step)
             last = min((g + 1) * GROUP, POSITIONS - step)
-            target = after_h[g, j][:, first - g * GROUP : last - g * GROUP]
-            nc.vector.scalar_tensor_tensor(
-                out=target, in0=after_d[j][:, first + step : last + step], scalar=tap(0, k, j), in1=target,
-                op0=MULT, op1=ADD,
-            )
+            target = rows_after_h(g, j)[:, (first - g * GROUP) // D_COLS : (last - g * GROUP) // D_COLS]
+            source = after_d[j][:, first + step : last + step].rearrange("p (r d) -> p r d", d=D_COLS)
+            add_tap(target, source, tap(H_AXIS, k, j), target)
 
-        def w_product(g, j, k):
+        def last_middle(j, engine):
+            d_sum[j] = sums.tile([P, ROWS, D_COLS], F32, name="d_sum")
+            times_tap(engine, d_sum[j][:], last_rows(j, 0), tap(D_AXIS, 1, j))
+
+        def last_outer(j, k):
+            if k == 0:
+                add_tap(d_sum[j][:], last_rows(j, -1), tap(D_AXIS, 0, j), d_sum[j][:])
+            else:
+                target = y3[:, j, :].rearrange("p (r d) -> p r d", d=D_COLS)
+                add_tap(target, last_rows(j, 1), tap(D_AXIS, 2, j), d_sum[j][:])
+
+        def last_regroup(half, engine):
+            if half == 0:
+                y_grouped[LAST] = work.tile([P, GROUP, PACK], BF16, name="y_grouped", align_bytes=64)
+            side_by_side(engine, y_grouped[LAST], y3, half * PLANE, (half + 1) * PLANE)
+
+        def w_product(g, j, k, engine):
             taken = (slice(0, D_COLS - 1), slice(0, D_COLS), slice(1, D_COLS))[k]
             put = (slice(1, D_COLS), slice(0, D_COLS), slice(0, D_COLS - 1))[k]
-            if k == 1 and j in DIAGONAL_CHUNKS:
+            if k == 1:
                 return
             target = scaled[g % 2][k][j][:, :, put]
             source = after_h[g, j][:].rearrange("p (r d) -> p r d", d=D_COLS)[:, :, taken]
-            if k == 1:
-                nc.scalar.activation(out=target, in_=source, func=COPY, scale=tap(2, k, j))
+            if engine == "scalar":
+                nc.scalar.activation(out=target, in_=source, func=COPY, scale=tap(D_AXIS, k, j))
             else:
-                nc.vector.tensor_scalar_mul(out=target, in0=source, scalar1=tap(2, k, j))
+                nc.vector.tensor_scalar_mul(out=target, in0=source, scalar1=tap(D_AXIS, k, j))
 
-        def add_and_turn(g, b):
-            by_position[g, b] = turn_banks.tile([P, CHANNELS], F32, name="by_position")
-            for j in range(CHUNKS):
+        def add_and_turn(g, b, chunks=tuple(range(CHUNKS)), pool=turn_banks, name="by_position"):
+            if 0 in chunks:
+                by_position[g, b] = pool.tile([P, CHANNELS], F32, name=name, tag=name)
+            for j in chunks:
                 for k in range(TAPS):
-                    if k == 1 and j in DIAGONAL_CHUNKS:
+                    if k == 1:
                         source, factor = after_h[g, j][:], diagonal[j]
                     else:
                         source, factor = scaled[g % 2][k][j][:].rearrange("p r d -> p (r d)"), ident_f32
@@ -256,7 +307,7 @@ def tile_lowrankconv3d_kernel(
         def round_y3(g, b, engine):
             pairs[g, b] = sums.tile([P, 2, 2 * P], BF16, name="pairs")
             target = pairs[g, b][:].rearrange("q u (p e) -> q u p e", e=2)
-            source = by_position[g, b][:].rearrange("q (p u e) -> q u p e", u=2, e=2)
+            source = by_position[g, b][:].rearrange("q (u e p) -> q u p e", u=2, e=2)
             if engine == "vector":
                 nc.vector.tensor_copy(out=target, in_=source)
             else:
@@ -306,8 +357,8 @@ def tile_lowrankconv3d_kernel(
             )
 
         def finish(g, i, engine):
-            result = sums.tile([P, GROUP], F32, name="result")
-            bias_column = table[:, BIAS_COLUMN + i : BIAS_COLUMN + i + 1]
+            result = sums.tile([P, GROUP], F32, name="result", bufs=8)
+            bias_column = bias_table[:, i : i + 1]
             if engine == "vector":
                 nc.vector.tensor_scalar_add(out=result[:], in0=out_bank[g, i][:], scalar1=bias_column)
             else:
@@ -324,39 +375,41 @@ def tile_lowrankconv3d_kernel(
 
         regroup_x(0, 0, "vector")
         regroup_x(0, 1, "scalar")
+        sort_u_in(0)
         quantise_x(0)
-        load_table()
-        fill_diagonals()
-        for j in range(CHUNKS):
+        nc.vector.tensor_copy(out=table[:], in_=tap_rows[:, :, 0 : TAPS * PACK])
+        for j in PAIRS[0]:
             first_product(0, j)
+        sort_u_in(1)
+        for j in PAIRS[1]:
+            first_product(0, j)
+        fill_diagonals()
+        for j in PAIRS[0]:
+            d_middle(0, j)
         regroup_x(1, 0, "vector")
         regroup_x(1, 1, "vector")
         quantise_x(1)
-        for j in PAIRS[0]:
-            d_middle(0, j)
+        nc.vector.tensor_copy(out=bias_table[:], in_=bias_rows[:])
 
-        for s in range(SLABS + 2):
+        for s in range(SLABS):
             g = s - 1
             c = s - 2
             f = s - 3
-            helper = "vector" if s >= SLABS else "scalar"
             if is_group(f):
                 quantise_y3(f)
             if is_group(c):
                 add_and_turn(c, 0)
                 add_and_turn(c, 1)
-            if is_slab(s):
-                for k in (0, 2):
-                    for j in PAIRS[0]:
-                        d_outer(s, j, k)
-                for j in PAIRS[1]:
-                    d_middle(s, j)
+            for k in (0, 2):
+                for j in PAIRS[0]:
+                    d_outer(s, j, k)
+            for j in PAIRS[1]:
+                d_middle(s, j)
             if is_slab(s + 2) and s > 0:
                 regroup_x(s + 2, 0, "gpsimd")
-            if is_slab(s):
-                for k in (0, 2):
-                    for j in PAIRS[1]:
-                        d_outer(s, j, k)
+            for k in (0, 2):
+                for j in PAIRS[1]:
+                    d_outer(s, j, k)
             if s == 0:
                 regroup_x(2, 0, "scalar")
                 regroup_x(2, 1, "scalar")
@@ -370,7 +423,7 @@ def tile_lowrankconv3d_kernel(
                 second_product(f, 1)
             if is_group(c):
                 round_y3(c, 0, "scalar")
-                round_y3(c, 1, helper)
+                round_y3(c, 1, "scalar")
             if is_group(g):
                 for k in (0, 2):
                     for j in PAIRS[0]:
@@ -384,7 +437,7 @@ def tile_lowrankconv3d_kernel(
                 add_and_turn(c, 3)
             if is_group(f):
                 finish(f, 0, "scalar")
-                finish(f, 1, helper)
+                finish(f, 1, "scalar")
             if is_group(g):
                 for k in (0, 2):
                     for j in PAIRS[1]:
@@ -396,26 +449,33 @@ def tile_lowrankconv3d_kernel(
                 for j in PAIRS[0]:
                     first_product(s + 1, j)
             if is_group(c):
-                regroup_y3(c, 0, helper)
+                regroup_y3(c, 0, "scalar")
                 round_y3(c, 2, "scalar")
-                round_y3(c, 3, helper)
-            if is_group(g):
+                round_y3(c, 3, "scalar")
+            if is_group(g) and g < LAST:
                 for j in PAIRS[0]:
-                    for k in range(TAPS):
-                        w_product(g, j, k)
+                    for k in (0, 2):
+                        w_product(g, j, k, "scalar" if False else "vector")
             if is_group(c):
                 turn_back(c, 2)
                 turn_back(c, 3)
             if is_group(f):
                 finish(f, 2, "scalar")
-                finish(f, 3, helper)
+                finish(f, 3, "scalar")
             if is_slab(s + 1):
                 for j in PAIRS[0]:
                     d_middle(s + 1, j)
-            if is_group(g):
+            if is_group(g) and g < LAST:
                 for j in PAIRS[1]:
-                    for k in range(TAPS):
-                        w_product(g, j, k)
+                    for k in (0, 2):
+                        w_product(g, j, k, "scalar" if k == 0 else "vector")
+            if g == LAST:
+                for j in range(CHUNKS):
+                    last_middle(j, "gpsimd" if j in PAIRS[0] else "scalar")
+                for pair in PAIRS:
+                    for k in (0, 2):
+                        for j in pair:
+                            last_outer(j, k)
             if is_slab(s + 1):
                 for j in PAIRS[1]:
                     first_product(s + 1, j)
@@ -423,3 +483,17 @@ def tile_lowrankconv3d_kernel(
                 regroup_y3(c, 1, "scalar")
             if is_slab(s + 2) and s > 0:
                 regroup_x(s + 2, 1, "gpsimd")
+
+        last_regroup(0, "vector")
+        quantise_y3(2)
+        last_regroup(1, "scalar")
+        for i in range(CHUNKS):
+            second_product(2, i)
+        quantise_y3(3)
+        finish(2, 0, "scalar")
+        finish(2, 1, "vector")
+        finish(2, 2, "scalar")
+        finish(2, 3, "vector")
+        for i in range(CHUNKS):
+            second_product(3, i)
+            finish(3, i, ("scalar", "vector")[i % 2])

@@ -29,6 +29,7 @@ TAPS = 3
 GAP = 8
 PADDED_ROW = GAP + D_COLS
 W_AXIS, H_AXIS, D_AXIS = 0, 1, 2
+LAST_SHARE = 352
 
 FLOPS = 2 * 2 * CHANNELS * CHANNELS * POSITIONS + (3 * (2 * TAPS - 1) + 1) * CHANNELS * POSITIONS
 
@@ -79,25 +80,28 @@ def tile_lowrankconv3d_kernel(
 
         def load_x(s):
             lo, hi = slab_bounds(s)
-            nc.sync.dma_start(out=x_raw[s][:], in_=x_rows[:, :, lo:hi])
+            queue = nc.scalar if s == 0 else nc.sync
+            queue.dma_start(out=x_raw[s][:], in_=x_rows[:, :, lo:hi])
 
-        tap_rows = keep.tile([P, 3, 16], BF16, name="tap_rows")
-        for axis, taps in enumerate((U_kw, U_kh, U_kd)):
-            nc.scalar.dma_start(
-                out=tap_rows[:, axis, 0 : TAPS * PACK].rearrange("p (k t) -> p k t", t=PACK),
-                in_=taps.rearrange("k (p t) -> p k t", t=PACK),
-            )
-        bias_rows = keep.tile([P, CHUNKS], BF16, name="bias_rows")
-        nc.scalar.dma_start(out=bias_rows[:], in_=bias.rearrange("(i m) -> m i", m=P))
-
-        load_x(0)
+        tap_rows = keep.tile([P, CHANNELS], BF16, name="tap_rows")
+        nc.vector.memset(tap_rows[:], 0.0)
+        bias_rows = keep.tile([P, P], BF16, name="bias_rows")
+        nc.vector.memset(bias_rows[:], 0.0)
+        zeros = keep.tile([P, 1], F32, name="zeros")
+        nc.vector.memset(zeros[:], 0.0)
         in_plane = load_scales(nc, keep, U_c_in_scales, "u_in")
+        load_x(0)
+        for axis, taps in enumerate((U_kw, U_kh, U_kd)):
+            nc.scalar.dma_start(out=tap_rows[axis * TAPS : (axis + 1) * TAPS, :], in_=taps)
         in_words = load_words(nc, keep, U_c_in_words, "u_in")
         for s in range(1, SLABS):
             load_x(s)
         out_plane = load_scales(nc, keep, U_c_out_scales, "u_out")
         out_words = load_words(nc, keep, U_c_out_words, "u_out")
+        nc.sync.dma_start(out=bias_rows[0:CHUNKS, :], in_=bias.rearrange("(i m) -> i m", m=P))
 
+        ident_bf16 = keep.tile([P, P], BF16, name="ident_bf16")
+        make_identity(nc, ident_bf16[:])
         ident_f32 = keep.tile([P, P], F32, name="ident_f32")
         make_identity(nc, ident_f32[:])
 
@@ -114,12 +118,25 @@ def tile_lowrankconv3d_kernel(
                 out=sorted_plane[:, chunks, :], in_=in_plane[:].rearrange("p (m t) -> p t m", t=CHUNKS)[:, chunks, :]
             )
 
-        table = keep.tile([P, 3, TAPS * PACK], F32, name="table")
+        TABLE_ROWS = 3 * TAPS
+        table = keep.tile([P, CHUNKS, TABLE_ROWS], F32, name="table")
         bias_table = keep.tile([P, CHUNKS], F32, name="bias_table")
 
+        def load_table():
+            bank = turn_banks.tile([P, CHUNKS, P], BF16, tag="by_position", name="table_bank")
+            by_rank = tap_rows[:].rearrange("r (m t) -> r t m", t=CHUNKS)
+            for t in range(CHUNKS):
+                nc.tensor.transpose(bank[:, t, :], by_rank[:, t, :], ident_bf16[:])
+            nc.vector.tensor_copy(out=table[:], in_=bank[:, :, 0:TABLE_ROWS])
+
+        def load_bias():
+            bank = turn_banks.tile([P, P], BF16, tag="by_position", name="bias_bank")
+            nc.tensor.transpose(bank[:], bias_rows[:], ident_bf16[:])
+            nc.vector.tensor_copy(out=bias_table[:], in_=bank[:, 0:CHUNKS])
+
         def tap(axis, k, t):
-            column = k * PACK + t
-            return table[:, axis, column : column + 1]
+            column = axis * TAPS + k
+            return table[:, t, column : column + 1]
 
         diagonal = {}
         for j in range(CHUNKS):
@@ -269,10 +286,10 @@ def tile_lowrankconv3d_kernel(
                 target = y3[:, j, :].rearrange("p (r d) -> p r d", d=D_COLS)
                 add_tap(target, last_rows(j, 1), tap(D_AXIS, 2, j), d_sum[j][:])
 
-        def last_regroup(half, engine):
-            if half == 0:
+        def last_regroup(lo, hi, engine):
+            if lo == 0:
                 y_grouped[LAST] = work.tile([P, GROUP, PACK], BF16, name="y_grouped", align_bytes=64)
-            side_by_side(engine, y_grouped[LAST], y3, half * PLANE, (half + 1) * PLANE)
+            side_by_side(engine, y_grouped[LAST], y3, lo, hi)
 
         def w_product(g, j, k, engine):
             taken = (slice(0, D_COLS - 1), slice(0, D_COLS), slice(1, D_COLS))[k]
@@ -373,11 +390,12 @@ def tile_lowrankconv3d_kernel(
         def is_group(g):
             return 0 <= g < GROUPS
 
+        nc.scalar.activation(out=zeros[:], in_=zeros[:], func=COPY)
         regroup_x(0, 0, "vector")
-        regroup_x(0, 1, "scalar")
-        sort_u_in(0)
+        regroup_x(0, 1, "vector")
         quantise_x(0)
-        nc.vector.tensor_copy(out=table[:], in_=tap_rows[:, :, 0 : TAPS * PACK])
+        load_table()
+        sort_u_in(0)
         for j in PAIRS[0]:
             first_product(0, j)
         sort_u_in(1)
@@ -386,34 +404,47 @@ def tile_lowrankconv3d_kernel(
         fill_diagonals()
         for j in PAIRS[0]:
             d_middle(0, j)
+        for k in (0, 2):
+            for j in PAIRS[0]:
+                d_outer(0, j, k)
         regroup_x(1, 0, "vector")
-        regroup_x(1, 1, "vector")
+        regroup_x(1, 1, "scalar")
+        for j in PAIRS[1]:
+            d_middle(0, j)
         quantise_x(1)
-        nc.vector.tensor_copy(out=bias_table[:], in_=bias_rows[:])
+        for j in PAIRS[0]:
+            first_product(1, j)
+        for j in PAIRS[0]:
+            d_middle(1, j)
+        for k in (0, 2):
+            for j in PAIRS[1]:
+                d_outer(0, j, k)
+        for j in PAIRS[1]:
+            first_product(1, j)
 
-        for s in range(SLABS):
+        for s in range(1, SLABS):
             g = s - 1
             c = s - 2
             f = s - 3
-            if is_group(f):
-                quantise_y3(f)
             if is_group(c):
                 add_and_turn(c, 0)
                 add_and_turn(c, 1)
             for k in (0, 2):
                 for j in PAIRS[0]:
                     d_outer(s, j, k)
+            if is_group(f):
+                quantise_y3(f)
             for j in PAIRS[1]:
                 d_middle(s, j)
-            if is_slab(s + 2) and s > 0:
+            if is_slab(s + 2):
                 regroup_x(s + 2, 0, "gpsimd")
+            if s == 1:
+                regroup_x(2, 0, "scalar")
+                regroup_x(2, 1, "scalar")
             for k in (0, 2):
                 for j in PAIRS[1]:
                     d_outer(s, j, k)
-            if s == 0:
-                regroup_x(2, 0, "scalar")
-                regroup_x(2, 1, "scalar")
-            if is_slab(s + 1) and s > 0:
+            if is_slab(s + 1):
                 quantise_x(s + 1)
             if is_group(g):
                 for j in PAIRS[0]:
@@ -424,6 +455,8 @@ def tile_lowrankconv3d_kernel(
             if is_group(c):
                 round_y3(c, 0, "scalar")
                 round_y3(c, 1, "scalar")
+            if s == 2:
+                load_bias()
             if is_group(g):
                 for k in (0, 2):
                     for j in PAIRS[0]:
@@ -431,9 +464,9 @@ def tile_lowrankconv3d_kernel(
                 for j in PAIRS[1]:
                     h_middle(g, j)
             if is_group(c):
+                add_and_turn(c, 2)
                 turn_back(c, 0)
                 turn_back(c, 1)
-                add_and_turn(c, 2)
                 add_and_turn(c, 3)
             if is_group(f):
                 finish(f, 0, "scalar")
@@ -442,6 +475,9 @@ def tile_lowrankconv3d_kernel(
                 for k in (0, 2):
                     for j in PAIRS[1]:
                         h_outer(g, j, k)
+            if g == LAST:
+                for j in PAIRS[0]:
+                    last_middle(j, "scalar")
             if is_group(f):
                 second_product(f, 2)
                 second_product(f, 3)
@@ -455,7 +491,7 @@ def tile_lowrankconv3d_kernel(
             if is_group(g) and g < LAST:
                 for j in PAIRS[0]:
                     for k in (0, 2):
-                        w_product(g, j, k, "scalar" if False else "vector")
+                        w_product(g, j, k, "scalar" if k == 0 and g == 0 else "vector")
             if is_group(c):
                 turn_back(c, 2)
                 turn_back(c, 3)
@@ -468,32 +504,31 @@ def tile_lowrankconv3d_kernel(
             if is_group(g) and g < LAST:
                 for j in PAIRS[1]:
                     for k in (0, 2):
-                        w_product(g, j, k, "scalar" if k == 0 else "vector")
-            if g == LAST:
-                for j in range(CHUNKS):
-                    last_middle(j, "gpsimd" if j in PAIRS[0] else "scalar")
-                for pair in PAIRS:
-                    for k in (0, 2):
-                        for j in pair:
-                            last_outer(j, k)
+                        w_product(g, j, k, "scalar" if k == 0 and g < 2 else "vector")
             if is_slab(s + 1):
                 for j in PAIRS[1]:
                     first_product(s + 1, j)
             if is_group(c):
                 regroup_y3(c, 1, "scalar")
-            if is_slab(s + 2) and s > 0:
+            if is_slab(s + 2):
                 regroup_x(s + 2, 1, "gpsimd")
 
-        last_regroup(0, "vector")
-        quantise_y3(2)
-        last_regroup(1, "scalar")
-        for i in range(CHUNKS):
-            second_product(2, i)
-        quantise_y3(3)
+        for j in PAIRS[1]:
+            last_middle(j, "vector")
+        for pair, k in ((PAIRS[0], 0), (PAIRS[0], 2), (PAIRS[1], 0), (PAIRS[1], 2)):
+            if pair == PAIRS[1] and k == 2:
+                quantise_y3(2)
+                for i in range(CHUNKS):
+                    second_product(2, i)
+            for j in pair:
+                last_outer(j, k)
         finish(2, 0, "scalar")
-        finish(2, 1, "vector")
-        finish(2, 2, "scalar")
-        finish(2, 3, "vector")
+        finish(2, 1, "scalar")
+        last_regroup(0, LAST_SHARE, "vector")
+        last_regroup(LAST_SHARE, GROUP, "scalar")
+        finish(2, 2, "vector")
+        quantise_y3(3)
+        finish(2, 3, "scalar")
         for i in range(CHUNKS):
             second_product(3, i)
-            finish(3, i, ("scalar", "vector")[i % 2])
+            finish(3, i, ("vector", "scalar")[i % 2])

@@ -83,60 +83,50 @@ def tile_lowrankconv3d_kernel(
             queue = nc.scalar if s == 0 else nc.sync
             queue.dma_start(out=x_raw[s][:], in_=x_rows[:, :, lo:hi])
 
-        tap_rows = keep.tile([P, CHANNELS], BF16, name="tap_rows")
-        nc.vector.memset(tap_rows[:], 0.0)
-        bias_rows = keep.tile([P, P], BF16, name="bias_rows")
-        nc.vector.memset(bias_rows[:], 0.0)
         zeros = keep.tile([P, 1], F32, name="zeros")
         nc.vector.memset(zeros[:], 0.0)
         in_plane = load_scales(nc, keep, U_c_in_scales, "u_in")
         load_x(0)
+        tap_rows = []
         for axis, taps in enumerate((U_kw, U_kh, U_kd)):
-            nc.scalar.dma_start(out=tap_rows[axis * TAPS : (axis + 1) * TAPS, :], in_=taps)
+            rows = keep.tile([P, TAPS * PACK], BF16, name="tap_rows%d" % axis)
+            nc.scalar.dma_start(
+                out=rows[:].rearrange("p (k t) -> p k t", t=PACK), in_=taps.rearrange("k (p t) -> p k t", t=PACK)
+            )
+            tap_rows.append(rows)
         in_words = load_words(nc, keep, U_c_in_words, "u_in")
         for s in range(1, SLABS):
             load_x(s)
         out_plane = load_scales(nc, keep, U_c_out_scales, "u_out")
         out_words = load_words(nc, keep, U_c_out_words, "u_out")
-        nc.sync.dma_start(out=bias_rows[0:CHUNKS, :], in_=bias.rearrange("(i m) -> i m", m=P))
+        bias_rows = keep.tile([P, CHUNKS], BF16, name="bias_rows")
+        nc.sync.dma_start(out=bias_rows[:], in_=bias.rearrange("(i m) -> m i", m=P))
 
-        ident_bf16 = keep.tile([P, P], BF16, name="ident_bf16")
-        make_identity(nc, ident_bf16[:])
         ident_f32 = keep.tile([P, P], F32, name="ident_f32")
         make_identity(nc, ident_f32[:])
 
         sorted_words = keep.tile([P, CHUNKS, P], U32, name="sorted_words", align_bytes=64)
         sorted_plane = keep.tile([P, CHUNKS, P], U8, name="sorted_plane", align_bytes=64)
 
-        def sort_u_in(p):
+        def sort_u_in(p, engine):
             chunks = slice(2 * p, 2 * p + 2)
-            nc.vector.tensor_copy(
+            engine.tensor_copy(
+                out=sorted_plane[:, chunks, :], in_=in_plane[:].rearrange("p (m t) -> p t m", t=CHUNKS)[:, chunks, :]
+            )
+            engine.tensor_copy(
                 out=sorted_words[:, chunks, :].bitcast(I32),
                 in_=in_words[:].bitcast(I32).rearrange("p (m t) -> p t m", t=CHUNKS)[:, chunks, :],
             )
-            nc.vector.tensor_copy(
-                out=sorted_plane[:, chunks, :], in_=in_plane[:].rearrange("p (m t) -> p t m", t=CHUNKS)[:, chunks, :]
-            )
 
-        TABLE_ROWS = 3 * TAPS
-        table = keep.tile([P, CHUNKS, TABLE_ROWS], F32, name="table")
+        table = []
+        for axis in range(3):
+            numbers = keep.tile([P, TAPS * PACK], F32, name="table%d" % axis)
+            table.append(numbers)
         bias_table = keep.tile([P, CHUNKS], F32, name="bias_table")
 
-        def load_table():
-            bank = turn_banks.tile([P, CHUNKS, P], BF16, tag="by_position", name="table_bank")
-            by_rank = tap_rows[:].rearrange("r (m t) -> r t m", t=CHUNKS)
-            for t in range(CHUNKS):
-                nc.tensor.transpose(bank[:, t, :], by_rank[:, t, :], ident_bf16[:])
-            nc.vector.tensor_copy(out=table[:], in_=bank[:, :, 0:TABLE_ROWS])
-
-        def load_bias():
-            bank = turn_banks.tile([P, P], BF16, tag="by_position", name="bias_bank")
-            nc.tensor.transpose(bank[:], bias_rows[:], ident_bf16[:])
-            nc.vector.tensor_copy(out=bias_table[:], in_=bank[:, 0:CHUNKS])
-
         def tap(axis, k, t):
-            column = axis * TAPS + k
-            return table[:, t, column : column + 1]
+            column = k * PACK + t
+            return table[axis][:, column : column + 1]
 
         diagonal = {}
         for j in range(CHUNKS):
@@ -394,19 +384,21 @@ def tile_lowrankconv3d_kernel(
         regroup_x(0, 0, "vector")
         regroup_x(0, 1, "vector")
         quantise_x(0)
-        load_table()
-        sort_u_in(0)
+        nc.vector.tensor_copy(out=table[W_AXIS][:], in_=tap_rows[W_AXIS][:])
+        sort_u_in(0, nc.vector)
         for j in PAIRS[0]:
             first_product(0, j)
-        sort_u_in(1)
+        sort_u_in(1, nc.vector)
         for j in PAIRS[1]:
             first_product(0, j)
-        fill_diagonals()
         for j in PAIRS[0]:
             d_middle(0, j)
         for k in (0, 2):
             for j in PAIRS[0]:
                 d_outer(0, j, k)
+        for axis in (H_AXIS, D_AXIS):
+            nc.vector.tensor_copy(out=table[axis][:], in_=tap_rows[axis][:])
+        fill_diagonals()
         regroup_x(1, 0, "vector")
         regroup_x(1, 1, "scalar")
         for j in PAIRS[1]:
@@ -456,7 +448,7 @@ def tile_lowrankconv3d_kernel(
                 round_y3(c, 0, "scalar")
                 round_y3(c, 1, "scalar")
             if s == 2:
-                load_bias()
+                nc.vector.tensor_copy(out=bias_table[:], in_=bias_rows[:])
             if is_group(g):
                 for k in (0, 2):
                     for j in PAIRS[0]:
@@ -491,7 +483,7 @@ def tile_lowrankconv3d_kernel(
             if is_group(g) and g < LAST:
                 for j in PAIRS[0]:
                     for k in (0, 2):
-                        w_product(g, j, k, "scalar" if k == 0 and g == 0 else "vector")
+                        w_product(g, j, k, "scalar" if k == 0 and g < 2 else "vector")
             if is_group(c):
                 turn_back(c, 2)
                 turn_back(c, 3)

@@ -503,7 +503,7 @@ def tile_lowrankconv3d_kernel(
             if is_group(c):
                 regroup_y3(c, 1, "scalar")
             if is_slab(s + 2):
-                regroup_x(s + 2, 1, "gpsimd")
+                regroup_x(s + 2, 1, "scalar")
 
         for j in PAIRS[1]:
             last_middle(j, "vector")

from contextlib import ExitStack

import concourse.mybir as mybir
from concourse.masks import make_identity

F32 = mybir.dt.float32
BF16 = mybir.dt.bfloat16
I32 = mybir.dt.int32
U32 = mybir.dt.uint32
U8 = mybir.dt.uint8
FP8X4 = mybir.dt.float8_e4m3fn_x4
MULT = mybir.AluOpType.mult
ADD = mybir.AluOpType.add
COPY = mybir.ActivationFunctionType.Copy
IDENTITY = mybir.ActivationFunctionType.Identity

P = 128
PACK = 4
CHANNELS = 512
CHUNKS = CHANNELS // P
H_PLANES, W_ROWS, D_COLS = 8, 16, 16
PLANE = W_ROWS * D_COLS
POSITIONS = H_PLANES * PLANE
GROUP = 2 * PLANE
GROUPS = POSITIONS // GROUP
SLABS = GROUPS + 1
ROWS = GROUP // D_COLS
TAPS = 3
GAP = 8
PADDED_ROW = GAP + D_COLS
W_AXIS, H_AXIS, D_AXIS = 0, 1, 2
LAST_SHARE = 352

FLOPS = 2 * 2 * CHANNELS * CHANNELS * POSITIONS + (3 * (2 * TAPS - 1) + 1) * CHANNELS * POSITIONS

def slab_bounds(s):
    return max(0, (2 * s - 1) * PLANE), min(POSITIONS, (2 * s + 1) * PLANE)


def load_scales(nc, pool, scales_dram, label):
    plane = pool.tile([P, CHANNELS], U8, name=label + "_plane", align_bytes=64)
    nc.vector.memset(plane[:].bitcast(I32), 0)
    for quadrant in range(4):
        nc.sync.dma_start(
            out=plane[32 * quadrant : 32 * quadrant + 4, :].bitcast(I32),
            in_=scales_dram[0, 4 * quadrant : 4 * quadrant + 4, :].bitcast(I32),
        )
    return plane


def load_words(nc, pool, words_dram, label):
    words = pool.tile([P, CHANNELS], U32, name=label + "_words", align_bytes=64)
    nc.sync.dma_start(
        out=words[:].bitcast(I32),
        in_=words_dram[0].rearrange("p n t -> p (n t)").bitcast(I32),
    )
    return words


def tile_lowrankconv3d_kernel(
    tc, x, U_kh, U_kw, U_kd, U_c_in_words, U_c_in_scales, U_c_out_words, U_c_out_scales, bias, out
):
    nc = tc.nc
    x_rows = x[0].rearrange("(p t) h w d -> p t (h w d)", t=PACK)
    out_rows = out[0].rearrange("(i m) h w d -> i m (h w d)", m=P)

    with ExitStack() as ctx:
        ctx.enter_context(tc.manual_schedule())
        keep = ctx.enter_context(tc.tile_pool(name="keep", bufs=1))
        work = ctx.enter_context(tc.tile_pool(name="work", bufs=2))
        sums = ctx.enter_context(tc.tile_pool(name="sums", bufs=4))
        product_banks = ctx.enter_context(tc.psum_pool(name="product_banks", bufs=4))
        turn_banks = ctx.enter_context(tc.psum_pool(name="turn_banks", bufs=3))
        last_banks = ctx.enter_context(tc.psum_pool(name="last_banks", bufs=1))

        x_raw = []
        for s in range(SLABS):
            lo, hi = slab_bounds(s)
            x_raw.append(keep.tile([P, PACK, hi - lo], BF16, name="x_raw%d" % s))

        def load_x(s):
            lo, hi = slab_bounds(s)
            queue = nc.scalar if s == 0 else nc.sync
            queue.dma_start(out=x_raw[s][:], in_=x_rows[:, :, lo:hi])

        zeros = keep.tile([P, 1], F32, name="zeros")
        nc.vector.memset(zeros[:], 0.0)
        in_plane = load_scales(nc, keep, U_c_in_scales, "u_in")
        load_x(0)
        tap_rows = []
        for axis, taps in enumerate((U_kw, U_kh, U_kd)):
            rows = keep.tile([P, TAPS * PACK], BF16, name="tap_rows%d" % axis)
            nc.scalar.dma_start(
                out=rows[:].rearrange("p (k t) -> p k t", t=PACK), in_=taps.rearrange("k (p t) -> p k t", t=PACK)
            )
            tap_rows.append(rows)
        in_words = load_words(nc, keep, U_c_in_words, "u_in")
        for s in range(1, SLABS):
            load_x(s)
        out_plane = load_scales(nc, keep, U_c_out_scales, "u_out")
        out_words = load_words(nc, keep, U_c_out_words, "u_out")
        bias_rows = keep.tile([P, CHUNKS], BF16, name="bias_rows")
        nc.sync.dma_start(out=bias_rows[:], in_=bias.rearrange("(i m) -> m i", m=P))

        ident_f32 = keep.tile([P, P], F32, name="ident_f32")
        make_identity(nc, ident_f32[:])

        sorted_words = keep.tile([P, CHUNKS, P], U32, name="sorted_words", align_bytes=64)
        sorted_plane = keep.tile([P, CHUNKS, P], U8, name="sorted_plane", align_bytes=64)

        def sort_u_in(p, engine):
            chunks = slice(2 * p, 2 * p + 2)
            engine.tensor_copy(
                out=sorted_plane[:, chunks, :], in_=in_plane[:].rearrange("p (m t) -> p t m", t=CHUNKS)[:, chunks, :]
            )
            engine.tensor_copy(
                out=sorted_words[:, chunks, :].bitcast(I32),
                in_=in_words[:].bitcast(I32).rearrange("p (m t) -> p t m", t=CHUNKS)[:, chunks, :],
            )

        table = []
        for axis in range(3):
            numbers = keep.tile([P, TAPS * PACK], F32, name="table%d" % axis)
            table.append(numbers)
        bias_table = keep.tile([P, CHUNKS], F32, name="bias_table")

        def tap(axis, k, t):
            column = k * PACK + t
            return table[axis][:, column : column + 1]

        diagonal = {}
        for j in range(CHUNKS):
            diagonal[j] = keep.tile([P, P], F32, name="diagonal%d" % j)

        def fill_diagonals():
            for j in range(CHUNKS):
                nc.gpsimd.tensor_scalar(
                    out=diagonal[j][:], in0=ident_f32[:], scalar1=tap(D_AXIS, 1, j), scalar2=0.0, op0=MULT, op1=ADD
                )

        after_d = []
        for j in range(CHUNKS):
            after_d.append(keep.tile([P, POSITIONS], F32, name="after_d%d" % j))
        scaled = []
        for parity in range(2):
            scaled.append([])
            for k in range(TAPS):
                scaled[parity].append([])
                for j in range(CHUNKS):
                    padded = keep.tile([P, ROWS, D_COLS], F32, name="scaled%d_%d_%d" % (parity, k, j))
                    scaled[parity][k].append(padded)
                    if k == 0:
                        nc.gpsimd.memset(padded[:, :, 0:4], 0.0)
                    if k == 2:
                        nc.gpsimd.memset(padded[:, :, D_COLS - 4 : D_COLS], 0.0)

        LAST = GROUPS - 1
        padded_rows = []
        for j in range(CHUNKS):
            padded = keep.tile([P, ROWS + 1, PADDED_ROW], F32, name="padded%d" % j)
            nc.gpsimd.memset(padded[:, :, 0:GAP], 0.0)
            padded_rows.append(padded)
        y3 = keep.tile([P, CHUNKS, GROUP], BF16, name="y3")

        def last_rows(j, shift):
            first = GAP + shift
            flat = padded_rows[j][:].rearrange("p r c -> p (r c)")[:, first : first + ROWS * PADDED_ROW]
            return flat.rearrange("p (r c) -> p r c", c=PADDED_ROW)[:, :, 0:D_COLS]

        def rows_after_h(g, j):
            if g == LAST:
                return last_rows(j, 0)
            return after_h[g, j][:].rearrange("p (r d) -> p r d", d=D_COLS)

        def copy(engine, target, source):
            if engine == "vector":
                nc.vector.tensor_copy(out=target, in_=source)
            elif engine == "gpsimd":
                nc.gpsimd.tensor_scalar(out=target, in0=source, scalar1=1.0, scalar2=0.0, op0=MULT, op1=ADD)
            else:
                nc.scalar.copy(out=target, in_=source)

        def times_tap(engine, target, source, factor):
            if engine == "gpsimd":
                nc.gpsimd.tensor_scalar(out=target, in0=source, scalar1=factor, scalar2=0.0, op0=MULT, op1=ADD)
            elif engine == "vector":
                nc.vector.tensor_scalar_mul(out=target, in0=source, scalar1=factor)
            else:
                nc.scalar.activation(out=target, in_=source, func=COPY, scale=factor)

        def add_tap(target, source, factor, total):
            nc.vector.scalar_tensor_tensor(out=target, in0=source, scalar=factor, in1=total, op0=MULT, op1=ADD)

        def side_by_side(engine, grouped, rows, lo, hi):
            copy(
                engine,
                grouped[:, lo:hi, :].rearrange("p (c i) t -> p c t i", i=4),
                rows[:, :, lo:hi].rearrange("p t (c i) -> p c t i", i=4),
            )

        x_grouped, x_codes, x_scales, y0, after_h = {}, {}, {}, {}, {}
        d_sum, by_position, pairs, by_word, y_grouped, y_codes, y_scales, out_bank = {}, {}, {}, {}, {}, {}, {}, {}

        PAIRS = ((0, 1), (2, 3))

        def regroup_x(s, part, engine):
            lo, hi = slab_bounds(s)
            n = (hi - lo) // 2
            if part == 0:
                x_grouped[s] = keep.tile([P, GROUP, PACK], BF16, name="x_grouped%d" % s, align_bytes=64)
            side_by_side(engine, x_grouped[s], x_raw[s], part * n, (part + 1) * n)

        def quantise_x(s):
            lo, hi = slab_bounds(s)
            n = hi - lo
            x_codes[s] = work.tile([P, GROUP], U32, name="x_codes", align_bytes=64)
            x_scales[s] = work.tile([P, GROUP], U8, name="x_scales", align_bytes=64)
            nc.vector.quantize_mx(
                out=x_codes[s][:, 0:n].bitcast(FP8X4),
                scales=x_scales[s][:, 0:n],
                in_=x_grouped[s][:, 0:n, :].rearrange("p q t -> p (q t)"),
            )

        def first_product(s, j):
            lo, hi = slab_bounds(s)
            n = hi - lo
            y0[s, j] = product_banks.tile([P, GROUP], F32, name="y0", tag="product")
            nc.tensor.matmul_mx(
                out=y0[s, j][:, 0:n],
                lhsT=sorted_words[:, j, :].bitcast(FP8X4),
                lhsT_scale=sorted_plane[:, j, :],
                rhs=x_codes[s][:, 0:n].bitcast(FP8X4),
                rhs_scale=x_scales[s][:, 0:n],
                start=True,
                stop=True,
            )

        def d_middle(s, j):
            lo, hi = slab_bounds(s)
            nc.scalar.activation(out=after_d[j][:, lo:hi], in_=y0[s, j][:, 0 : hi - lo], func=COPY, scale=tap(W_AXIS, 1, j))

        def d_outer(s, j, k):
            lo, hi = slab_bounds(s)
            source = y0[s, j][:, 0 : hi - lo].rearrange("p (h q) -> p h q", q=PLANE)
            target = after_d[j][:, lo:hi].rearrange("p (h q) -> p h q", q=PLANE)
            if k == 0:
                source, target = source[:, :, 0 : PLANE - D_COLS], target[:, :, D_COLS:PLANE]
            else:
                source, target = source[:, :, D_COLS:PLANE], target[:, :, 0 : PLANE - D_COLS]
            nc.vector.scalar_tensor_tensor(
                out=target, in0=source, scalar=tap(W_AXIS, k, j), in1=target, op0=MULT, op1=ADD
            )

        def h_middle(g, j):
            if g < LAST:
                after_h[g, j] = sums.tile([P, GROUP], F32, name="after_h", bufs=8)
            source = after_d[j][:, g * GROUP : (g + 1) * GROUP].rearrange("p (r d) -> p r d", d=D_COLS)
            times_tap("gpsimd" if j in PAIRS[0] else "scalar", rows_after_h(g, j), source, tap(H_AXIS, 1, j))

        def h_outer(g, j, k):
            step = (k - 1) * PLANE
            first = max(g * GROUP, -step)
            last = min((g + 1) * GROUP, POSITIONS - step)
            target = rows_after_h(g, j)[:, (first - g * GROUP) // D_COLS : (last - g * GROUP) // D_COLS]
            source = after_d[j][:, first + step : last + step].rearrange("p (r d) -> p r d", d=D_COLS)
            add_tap(target, source, tap(H_AXIS, k, j), target)

        def last_middle(j, engine):
            d_sum[j] = sums.tile([P, ROWS, D_COLS], F32, name="d_sum")
            times_tap(engine, d_sum[j][:], last_rows(j, 0), tap(D_AXIS, 1, j))

        def last_outer(j, k):
            if k == 0:
                add_tap(d_sum[j][:], last_rows(j, -1), tap(D_AXIS, 0, j), d_sum[j][:])
            else:
                target = y3[:, j, :].rearrange("p (r d) -> p r d", d=D_COLS)
                add_tap(target, last_rows(j, 1), tap(D_AXIS, 2, j), d_sum[j][:])

        def last_regroup(lo, hi, engine):
            if lo == 0:
                y_grouped[LAST] = work.tile([P, GROUP, PACK], BF16, name="y_grouped", align_bytes=64)
            side_by_side(engine, y_grouped[LAST], y3, lo, hi)

        def w_product(g, j, k, engine):
            taken = (slice(0, D_COLS - 1), slice(0, D_COLS), slice(1, D_COLS))[k]
            put = (slice(1, D_COLS), slice(0, D_COLS), slice(0, D_COLS - 1))[k]
            if k == 1:
                return
            target = scaled[g % 2][k][j][:, :, put]
            source = after_h[g, j][:].rearrange("p (r d) -> p r d", d=D_COLS)[:, :, taken]
            if engine == "scalar":
                nc.scalar.activation(out=target, in_=source, func=COPY, scale=tap(D_AXIS, k, j))
            else:
                nc.vector.tensor_scalar_mul(out=target, in0=source, scalar1=tap(D_AXIS, k, j))

        def add_and_turn(g, b, chunks=tuple(range(CHUNKS)), pool=turn_banks, name="by_position"):
            if 0 in chunks:
                by_position[g, b] = pool.tile([P, CHANNELS], F32, name=name, tag=name)
            for j in chunks:
                for k in range(TAPS):
                    if k == 1:
                        source, factor = after_h[g, j][:], diagonal[j]
                    else:
                        source, factor = scaled[g % 2][k][j][:].rearrange("p r d -> p (r d)"), ident_f32
                    nc.tensor.matmul(
                        out=by_position[g, b][:, j * P : (j + 1) * P],
                        lhsT=source[:, b * P : (b + 1) * P],
                        rhs=factor[:],
                        start=(k == 0),
                        stop=(k == TAPS - 1),
                        is_transpose=factor is ident_f32,
                    )

        def round_y3(g, b, engine):
            pairs[g, b] = sums.tile([P, 2, 2 * P], BF16, name="pairs")
            target = pairs[g, b][:].rearrange("q u (p e) -> q u p e", e=2)
            source = by_position[g, b][:].rearrange("q (u e p) -> q u p e", u=2, e=2)
            if engine == "vector":
                nc.vector.tensor_copy(out=target, in_=source)
            else:
                nc.scalar.copy(out=target, in_=source)

        def turn_back(g, b):
            if b % 2 == 0:
                by_word[g, b // 2] = last_banks.tile([P, 2, 2, P], F32, name="by_word")
            for u in range(2):
                nc.tensor.transpose(
                    by_word[g, b // 2][:, b % 2, u, :], pairs[g, b][:, u, :].bitcast(F32), ident_f32[:]
                )

        def regroup_y3(g, half, engine):
            if half == 0:
                y_grouped[g] = work.tile([P, GROUP, PACK], BF16, name="y_grouped", align_bytes=64)
            grouped_pairs = (
                y_grouped[g][:].rearrange("p q t -> p (q t)").bitcast(F32).rearrange("p (q u) -> p q u", u=2)
            )
            target = grouped_pairs[:, 2 * half * P : 2 * (half + 1) * P, :].rearrange("p (b q) u -> p b q u", b=2)
            source = by_word[g, half][:].rearrange("p b u q -> p b q u")
            if engine == "vector":
                nc.vector.tensor_copy(out=target, in_=source)
            else:
                nc.scalar.copy(out=target, in_=source)

        def quantise_y3(g):
            y_codes[g] = work.tile([P, GROUP], U32, name="y_codes", align_bytes=64)
            y_scales[g] = work.tile([P, GROUP], U8, name="y_scales", align_bytes=64)
            nc.vector.quantize_mx(
                out=y_codes[g][:].bitcast(FP8X4),
                scales=y_scales[g][:],
                in_=y_grouped[g][:].rearrange("p q t -> p (q t)"),
            )

        def second_product(g, i):
            channels = slice(i * P, (i + 1) * P)
            out_bank[g, i] = product_banks.tile([P, GROUP], F32, name="out_bank", tag="product")
            nc.tensor.matmul_mx(
                out=out_bank[g, i][:],
                lhsT=out_words[:, channels].bitcast(FP8X4),
                lhsT_scale=out_plane[:, channels],
                rhs=y_codes[g][:].bitcast(FP8X4),
                rhs_scale=y_scales[g][:],
                start=True,
                stop=True,
            )

        def finish(g, i, engine):
            result = sums.tile([P, GROUP], F32, name="result", bufs=8)
            bias_column = bias_table[:, i : i + 1]
            if engine == "vector":
                nc.vector.tensor_scalar_add(out=result[:], in0=out_bank[g, i][:], scalar1=bias_column)
            else:
                nc.scalar.activation(
                    out=result[:], in_=out_bank[g, i][:], func=IDENTITY, bias=bias_column, scale=1.0
                )
            nc.sync.dma_start(out=out_rows[i, :, g * GROUP : (g + 1) * GROUP], in_=result[:])

        def is_slab(s):
            return 0 <= s < SLABS

        def is_group(g):
            return 0 <= g < GROUPS

        nc.scalar.activation(out=zeros[:], in_=zeros[:], func=COPY)
        regroup_x(0, 0, "vector")
        regroup_x(0, 1, "vector")
        quantise_x(0)
        nc.vector.tensor_copy(out=table[W_AXIS][:], in_=tap_rows[W_AXIS][:])
        sort_u_in(0, nc.vector)
        for j in PAIRS[0]:
            first_product(0, j)
        sort_u_in(1, nc.vector)
        for j in PAIRS[1]:
            first_product(0, j)
        for j in PAIRS[0]:
            d_middle(0, j)
        for k in (0, 2):
            for j in PAIRS[0]:
                d_outer(0, j, k)
        for axis in (H_AXIS, D_AXIS):
            nc.vector.tensor_copy(out=table[axis][:], in_=tap_rows[axis][:])
        fill_diagonals()
        regroup_x(1, 0, "vector")
        regroup_x(1, 1, "scalar")
        for j in PAIRS[1]:
            d_middle(0, j)
        quantise_x(1)
        for j in PAIRS[0]:
            first_product(1, j)
        for j in PAIRS[0]:
            d_middle(1, j)
        for k in (0, 2):
            for j in PAIRS[1]:
                d_outer(0, j, k)
        for j in PAIRS[1]:
            first_product(1, j)

        for s in range(1, SLABS):
            g = s - 1
            c = s - 2
            f = s - 3
            if is_group(c):
                add_and_turn(c, 0)
                add_and_turn(c, 1)
            for k in (0, 2):
                for j in PAIRS[0]:
                    d_outer(s, j, k)
            if is_group(f):
                quantise_y3(f)
            for j in PAIRS[1]:
                d_middle(s, j)
            if is_slab(s + 2):
                regroup_x(s + 2, 0, "gpsimd")
            if s == 1:
                regroup_x(2, 0, "scalar")
                regroup_x(2, 1, "scalar")
            for k in (0, 2):
                for j in PAIRS[1]:
                    d_outer(s, j, k)
            if is_slab(s + 1):
                quantise_x(s + 1)
            if is_group(g):
                for j in PAIRS[0]:
                    h_middle(g, j)
            if is_group(f):
                second_product(f, 0)
                second_product(f, 1)
            if is_group(c):
                round_y3(c, 0, "scalar")
                round_y3(c, 1, "scalar")
            if s == 2:
                nc.vector.tensor_copy(out=bias_table[:], in_=bias_rows[:])
            if is_group(g):
                for k in (0, 2):
                    for j in PAIRS[0]:
                        h_outer(g, j, k)
                for j in PAIRS[1]:
                    h_middle(g, j)
            if is_group(c):
                add_and_turn(c, 2)
                turn_back(c, 0)
                turn_back(c, 1)
                add_and_turn(c, 3)
            if is_group(f):
                finish(f, 0, "scalar")
                finish(f, 1, "scalar")
            if is_group(g):
                for k in (0, 2):
                    for j in PAIRS[1]:
                        h_outer(g, j, k)
            if g == LAST:
                for j in PAIRS[0]:
                    last_middle(j, "scalar")
            if is_group(f):
                second_product(f, 2)
                second_product(f, 3)
            if is_slab(s + 1):
                for j in PAIRS[0]:
                    first_product(s + 1, j)
            if is_group(c):
                regroup_y3(c, 0, "scalar")
                round_y3(c, 2, "scalar")
                round_y3(c, 3, "scalar")
            if is_group(g) and g < LAST:
                for j in PAIRS[0]:
                    for k in (0, 2):
                        w_product(g, j, k, "scalar" if k == 0 and g < 2 else "vector")
            if is_group(c):
                turn_back(c, 2)
                turn_back(c, 3)
            if is_group(f):
                finish(f, 2, "scalar")
                finish(f, 3, "scalar")
            if is_slab(s + 1):
                for j in PAIRS[0]:
                    d_middle(s + 1, j)
            if is_group(g) and g < LAST:
                for j in PAIRS[1]:
                    for k in (0, 2):
                        w_product(g, j, k, "scalar" if k == 0 and g < 2 else "vector")
            if is_slab(s + 1):
                for j in PAIRS[1]:
                    first_product(s + 1, j)
            if is_group(c):
                regroup_y3(c, 1, "scalar")
            if is_slab(s + 2):
                regroup_x(s + 2, 1, "scalar")

        for j in PAIRS[1]:
            last_middle(j, "vector")
        for pair, k in ((PAIRS[0], 0), (PAIRS[0], 2), (PAIRS[1], 0), (PAIRS[1], 2)):
            if pair == PAIRS[1] and k == 2:
                quantise_y3(2)
                for i in range(CHUNKS):
                    second_product(2, i)
            for j in pair:
                last_outer(j, k)
        finish(2, 0, "scalar")
        finish(2, 1, "scalar")
        last_regroup(0, LAST_SHARE, "vector")
        last_regroup(LAST_SHARE, GROUP, "scalar")
        finish(2, 2, "vector")
        quantise_y3(3)
        finish(2, 3, "scalar")
        for i in range(CHUNKS):
            second_product(3, i)
            finish(3, i, ("vector", "scalar")[i % 2])
